import numpy as np
import ml_dtypes


def mxq(x, axis, fmt="e4m3"):
    dtype, down = {"e4m3": (ml_dtypes.float8_e4m3fn, 7), "e5m2": (ml_dtypes.float8_e5m2, 14)}[fmt]
    v = np.moveaxis(np.asarray(x, np.float32).astype(ml_dtypes.bfloat16).astype(np.float64), axis, -1)
    blocks = v.reshape(v.shape[:-1] + (-1, 32))
    amax = np.abs(blocks).max(-1, keepdims=True)
    byte = np.maximum(np.where(amax > 0, np.frexp(amax)[1] - 1 + 127, 0) - down, 1)
    scale = np.exp2(byte - 127.0)
    codes = (blocks / scale).astype(np.float32).astype(dtype).astype(np.float64)
    return np.moveaxis((codes * scale).reshape(v.shape), -1, axis)


WIDE = False


def mx_kscale(k):
    if not WIDE:
        return np.ones(k)
    levels = np.array([18, -18])
    if k % 512:
        return np.exp2(np.random.permutation(np.resize(levels, k // 32))).repeat(32)
    a = np.empty((k // 512, 16))
    for p in range(k // 512):
        a[p, :8] = np.random.permutation(np.resize(levels, 8))
        for g in range(8):
            far = levels[np.abs(levels - a[p, g]) >= 10]
            a[p, g + 8] = far[np.random.randint(len(far))]
    return np.exp2(a.ravel()).repeat(32)


BF16 = ml_dtypes.bfloat16


def bf(x):
    return np.asarray(x, np.float32).astype(BF16)


def f64(x):
    return np.asarray(x).astype(np.float64)


B, I, H = 1024, 512, 1024
C = I + H


def hard_sigmoid(v):
    return np.clip(v / 6.0 + 0.5, 0.0, 1.0)


def hard_tanh(v):
    return np.clip(v, -1.0, 1.0)


def clear_of_edges(y, b, edge):
    b = f64(b)
    for _ in range(50):
        near = (np.abs(np.abs(y + b) - edge) < 2e-4).any(axis=0)
        if not near.any():
            break
        b = np.where(near, f64(bf(b + 0.0625)), b)
    return bf(b)


def setup_inputs():
    s = mx_kscale(B)[:, None]
    u = mx_kscale(H)
    v = mx_kscale(H)
    n = 1.0 / np.max(s) ** 2
    x0 = bf(np.random.standard_normal((B, I)))
    h0 = bf(np.random.standard_normal((B, H)))
    wz0 = bf(np.random.standard_normal((H, C)) * 2.5 / np.sqrt(C))
    b_z = bf(np.random.standard_normal(H) * 1.0)
    wr0 = bf(np.random.standard_normal((H, C)) * 2.5 / np.sqrt(C))
    b_r = bf(np.random.standard_normal(H) * 1.0)
    wh0 = bf(np.random.standard_normal((H, C)) * 1.2 / np.sqrt(C))
    b_h = bf(np.random.standard_normal(H) * 0.5)
    g = bf(4.0 * np.random.standard_normal((B, H)) * np.exp2(np.random.randint(-6, 1, (B, 1))) * u * n)
    ih = np.concatenate([f64(x0), f64(h0)], axis=1)
    y_z = ih @ f64(wz0).T
    b_z = clear_of_edges(y_z, b_z, 3.0)
    a_z = y_z + f64(b_z)
    y_r = ih @ f64(wr0).T
    b_r = clear_of_edges(y_r, b_r, 3.0)
    a_r = y_r + f64(b_r)
    irh = np.concatenate([f64(x0), hard_sigmoid(a_r) * f64(h0)], axis=1)
    y_h = irh @ f64(wh0).T
    b_h = clear_of_edges(y_h, b_h, 1.0)
    a_h = y_h + f64(b_h)
    vc = np.concatenate([np.ones(I), v])
    return {"inputs": bf(f64(x0) / s / n),
            "h_prev": bf(f64(h0) * s),
            "W_z": bf(f64(wz0) / u[:, None]),
            "b_z": b_z,
            "W_r": bf(f64(wr0) / v[:, None]),
            "b_r": b_r,
            "W_h": bf(f64(wh0) * vc / u[:, None]),
            "b_h": b_h,
            "a_z": np.asarray(a_z, np.float32),
            "a_r": np.asarray(a_r, np.float32),
            "a_h": np.asarray(a_h, np.float32),
            "grad_out": g}


def reference(inputs, h_prev, W_z, b_z, W_r, b_r, W_h, b_h, a_z, a_r, a_h, grad_out):
    h, g = f64(h_prev), f64(grad_out)
    az, ar, ah = f64(a_z), f64(a_r), f64(a_h)
    z, r, h_tilde = hard_sigmoid(az), hard_sigmoid(ar), hard_tanh(ah)
    dz2 = g * (1.0 - z) * np.where(np.abs(ah) < 1.0, 1.0, 0.0)
    d_rh = mxq(dz2, 1, "e5m2") @ mxq(f64(W_h)[:, I:], 0, "e4m3")
    da_r = d_rh * h * np.where(np.abs(ar) < 3.0, 1.0 / 6.0, 0.0)
    da_z = g * (h - h_tilde) * np.where(np.abs(az) < 3.0, 1.0 / 6.0, 0.0)
    dgates = np.concatenate([da_z, da_r], axis=1)
    w_gates = np.concatenate([f64(W_z)[:, I:], f64(W_r)[:, I:]], axis=0)
    dh_prev = (mxq(dgates, 1, "e5m2") @ mxq(w_gates, 0, "e4m3")) + g * z + d_rh * r
    ih = np.concatenate([f64(inputs), h], axis=1)
    dW_r = mxq(da_r, 0, "e5m2").T @ mxq(ih, 0, "e4m3")
    return dh_prev, dW_r

@@ -1,0 +1,475 @@
+from contextlib import ExitStack
+import math
+
+import concourse.mybir as mybir
+from concourse.masks import make_identity
+
+F32 = mybir.dt.float32
+BF16 = mybir.dt.bfloat16
+U32 = mybir.dt.uint32
+U8 = mybir.dt.uint8
+E4M3X4 = mybir.dt.float8_e4m3fn_x4
+E5M2X4 = mybir.dt.float8_e5m2_x4
+ACT = mybir.ActivationFunctionType
+ALU = mybir.AluOpType
+
+B, I, H = 1024, 512, 1024
+C = I + H
+FLOPS = 2 * B * H * H + 2 * B * 2 * H * H + 2 * H * B * C
+BYTES = 2 * (B * I + B * H + 3 * H * H + B * H) + 4 * 3 * B * H + 4 * (B * H + H * C)
+
+P = 128
+PACK = 4
+NB = 512
+TILES = 8
+KP = 2
+
+SIXTH = 1.0 / 6.0
+EDGE = 1.0 + 2.0 ** -8
+ROOT_1 = math.sqrt(EDGE) * (1.0 + 2.0 ** -22)
+ROOT_3 = ROOT_1 / 3.0
+
+AZB, B2K = 3, 6
+
+
+def il_cut(key, c0, c1, step=256):
+    return [("il", key, c, min(c + step, c1)) for c in range(c0, c1, step)]
+
+
+def in_cut(g):
+    return [("ilin", g, c, c + 256) for c in (0, 256)]
+
+
+LOADS = {(1,): [("load", ("h", 1))], (4,): [("load", "in")], (5,): [("load", ("z", 0))], (7,): [("load", ("z", 1))], ("u", 1): [("load", ("r", 0))], ("u", 3): [("load", ("r", 1))]}
+V1 = {
+    (0, 0): [("new", ("h", 0))] + il_cut(("h", 0), 0, 512, 512),
+    (0, 1): il_cut(("h", 0), 512, 1024, 512),
+    (1, 0): [("qw", ("h", 0))],
+    (2, 0): [("new", ("h", 1))] + il_cut(("h", 1), 0, 512, 512),
+    (3, 0): il_cut(("h", 1), 512, 1024, 512), (4, 0): [("qw", ("h", 1))],
+    (6, 0): [("qin", 0), ("qin", 1)],
+    (7, 1): [("qh", 0, 0, 1024)],
+    (8, 1): [("new", ("z", 0))] + il_cut(("z", 0), 0, 1024, 512),
+}
+S1 = {
+    (5, 0): [("new", "in")] + in_cut(0), (5, 1): in_cut(1),
+    (6, 0): [("new", "h0")] + il_cut("h0", 0, 256), (6, 1): il_cut("h0", 256, 512),
+    (7, 0): il_cut("h0", 512, 1024),
+    (8, 0): [("new", "h1")] + il_cut("h1", 0, 512),
+}
+V2 = {
+    (0, 2): [("qw", ("z", 0)), ("qh", 1, 0, 1024)],
+    (2, 2): [("new", ("z", 1))] + il_cut(("z", 1), 0, 1024, 512) + [("qw", ("z", 1)), ("qd", 0, 0, 0, 512)],
+    (4, 0): il_cut(("d", 1, 0), 0, 256),
+    (4, 2): [("qd", 1, 0, 0, 256), ("qd", 1, 0, 256, 512)],
+    (4, 1): [("qw", ("r", 0))],
+    (5, 2): [("qw", ("r", 1)), ("out0", 0), ("out0", 1)],
+    (6, 0): [("out", 0), ("out", 1)],
+    (6, 2): [("out0", 2), ("out0", 3)],
+    (7, 0): [("out", 2), ("out", 3)],
+    (7, 2): [("qd", 0, 1, 0, 512), ("out0", 4), ("out0", 5)],
+    (8, 0): il_cut(("d", 1, 1), 0, 256) + [("out", 4), ("out", 5), ("qd", 1, 1, 0, 256)],
+    (8, 2): [("qd", 1, 1, 256, 512), ("out0", 6), ("out", 6), ("out0", 7), ("out", 7)],
+}
+S2 = {
+    (0, 0): il_cut("h1", 512, 1024),
+    (2, 1): [("new", ("d", 0, 0))] + il_cut(("d", 0, 0), 0, 512),
+    (3, 0): [("new", ("r", 0))] + il_cut(("r", 0), 0, 512), (3, 1): il_cut(("r", 0), 512, 1024),
+    (4, 0): [("new", ("d", 1, 0))] + il_cut(("d", 1, 0), 256, 512),
+    (4, 1): [("new", ("r", 1))] + il_cut(("r", 1), 0, 512),
+    (5, 0): il_cut(("r", 1), 512, 1024),
+    (5, 1): [("x", 0, 4)],
+    (6, 0): [("new", ("d", 0, 1))] + il_cut(("d", 0, 1), 0, 256), (6, 1): il_cut(("d", 0, 1), 256, 512) + [("x", 4, 8)],
+    (7, 1): [("x", 8, 12)],
+    (8, 0): [("new", ("d", 1, 1))] + il_cut(("d", 1, 1), 256, 512),
+    (8, 2): [("x", 12, 24)],
+}
+
+
+def tile_grucell_v_kernel(
+    tc, inputs, h_prev, W_z, b_z, W_r, b_r, W_h, b_h, a_z, a_r, a_h, grad_out, out_0, out_1
+):
+    nc = tc.nc
+    V, S, G, PE, Q = nc.vector, nc.scalar, nc.gpsimd, nc.tensor, nc.sync
+
+    def tokens(x):
+        return x.rearrange("(g p j) w -> p g j w", g=KP, j=PACK)
+
+    az_h, ar_h, ah_h = tokens(a_z), tokens(a_r), tokens(a_h)
+    g_h, h_h, in_h, o0_h = tokens(grad_out), tokens(h_prev), tokens(inputs), tokens(out_0)
+    w_h = {n: w[:, I:].rearrange("(k p j) c -> p k j c", k=KP, j=PACK) for n, w in (("h", W_h), ("z", W_z), ("r", W_r))}
+
+    with ExitStack() as ctx:
+        pool = ctx.enter_context(tc.tile_pool(name="sb", bufs=1))
+        psum = ctx.enter_context(tc.psum_pool(name="ps", bufs=1))
+
+        def sb(shape, dt, tag, bufs=1):
+            return pool.tile(shape, dt, name=tag, tag=tag, bufs=bufs, align_bytes=64)
+
+        def f4k(shape, tag, bufs):
+            return sb(shape, F32, tag, bufs)
+
+        def b2k(shape):
+            return sb(shape, BF16, "b2k", B2K)
+
+        def bank(tag, bufs):
+            return psum.tile([P, NB], F32, name=tag, tag=tag, bufs=bufs)
+
+        half = sb([P, 1], F32, "half")
+        ident = sb([P, P], F32, "ident")
+        V.memset(half[:], 0.5)
+        make_identity(nc, ident[:])
+
+        wq = {n: (sb([P, KP, H], U32, "wq" + n), sb([P, KP, H], U8, "ws" + n)) for n in "hzr"}
+        iq, isc = sb([P, KP, C], U32, "iq"), sb([P, KP, C], U8, "isc")
+        dq, dsc = sb([P, KP, H], U32, "dq"), sb([P, KP, H], U8, "dsc")
+        aq, asc = sb([P, TILES, KP * P], U32, "aq"), sb([P, TILES, KP * P], U8, "asc")
+        bq, bsc = sb([P, TILES, KP * P], U32, "bq"), sb([P, TILES, KP * P], U8, "bsc")
+        fq = [sb([P, TILES, P], U32, "fq%d" % n) for n in range(KP)]
+        fsc = [sb([P, TILES, P], U8, "fsc%d" % n) for n in range(KP)]
+        hg = [sb([P, PACK, H], BF16, "hg%d" % g) for g in range(KP)]
+        ut = [sb([P, H], F32, "u%d" % i) for i in range(TILES)]
+
+        az, ah, gg, raw, gr = {}, {}, {}, {}, {}
+        qh, gm, ab, aT, gT, bT, dT = {}, {}, {}, {}, {}, {}, {}
+        htp, nhp, e_ps, tr = {}, {}, {}, {}
+        arh, hm, dn, d_ps, o_ps = {}, {}, {}, {}, {}
+
+        def load_w(n, kp):
+            raw[n, kp] = sb([P, PACK, H], BF16, "raw", 2)
+            Q.dma_start(out=raw[n, kp][:], in_=w_h[n][:, kp])
+
+        def load_in():
+            raw["in"] = sb([P, KP, PACK, I], BF16, "raw", 2)
+            Q.dma_start(out=raw["in"][:], in_=in_h)
+
+        def load_az(i):
+            az[i] = f4k([P, H], "az", AZB)
+            Q.dma_start(out=az[i][:], in_=az_h[:, i // 4, i % 4, :])
+
+        def load_ah(i):
+            ah[i] = f4k([P, H], "ah", 3)
+            Q.dma_start(out=ah[i][:], in_=ah_h[:, i // 4, i % 4, :])
+
+        def load_g(i):
+            gg[i] = sb([P, H], BF16, "gg", 3)
+            Q.dma_start(out=gg[i][:], in_=g_h[:, i // 4, i % 4, :])
+
+        def load_h(i):
+            Q.dma_start(out=hg[i // 4][:, i % 4, :], in_=h_h[:, i // 4, i % 4, :])
+
+        def load_ar(j):
+            q, n = j % 4, j // 4
+            g, t = q // 2, 2 * (q % 2)
+            arh[j] = f4k([P, 2, NB], "ah", 3)
+            Q.dma_start(out=arh[j][:], in_=ar_h[:, g, t:t + 2, n * NB:(n + 1) * NB])
+
+        def cols(n):
+            return slice(n * NB, (n + 1) * NB)
+
+        def s_p(i):
+            S.activation(out=ut[i][:], in_=az[i][:], func=ACT.Relu, bias=half[:], scale=-SIXTH)
+
+        def s_qh(i):
+            qh[i] = b2k([P, H])
+            S.activation(out=qh[i][:], in_=ah[i][:], func=ACT.Square, scale=ROOT_1)
+
+        def s_qz(i):
+            gm[i] = b2k([P, H])
+            S.activation(out=gm[i][:], in_=az[i][:], func=ACT.Square, scale=ROOT_3)
+
+        def by_slot(x):
+            return x.rearrange("p (k m t) -> p k m t", k=KP, t=PACK)
+
+        def s_nh(i):
+            nhp[i] = f4k([P, KP, PACK, P], "nh", 1)
+            S.activation(out=nhp[i][:].rearrange("p k t m -> p k m t"), in_=by_slot(hg[i // 4][:, i % 4, :]), func=ACT.Copy, scale=-1.0)
+
+        def words(key, src):
+            tr[key] = psum.tile([P, KP * 2, P], F32, name="tr", tag="tr", bufs=2)
+            w = src.bitcast(F32)
+            for kp in range(KP):
+                for u in range(2):
+                    PE.transpose(tr[key][:, 2 * kp + u, :], w[:, 256 * kp + u:256 * (kp + 1):2], ident[:])
+
+        def s_words(key):
+            out = sb([P, KP, P, PACK], BF16, "T" + key[0], 1)
+            S.copy(out=out[:].bitcast(F32), in_=tr[key][:].rearrange("p (k u) r -> p k r u", k=KP))
+            return out
+
+        def quant(codes, scales, src, fmt):
+            V.quantize_mx(out=codes.bitcast(fmt), scales=scales, in_=src)
+
+        def v_u(i):
+            V.scalar_tensor_tensor(out=ut[i][:], in0=ut[i][:], scalar=1.0, in1=gg[i][:], op0=ALU.min, op1=ALU.mult)
+
+        def v_A(i):
+            a = b2k([P, H])
+            V.scalar_tensor_tensor(out=a[:], in0=qh[i][:], scalar=EDGE, in1=ut[i][:], op0=ALU.is_lt, op1=ALU.mult)
+            words(("a", i), a[:])
+
+        def gz(eng, i, n):
+            eng.tensor_tensor(out=ut[i][:, cols(n)], in0=gg[i][:, cols(n)], in1=ut[i][:, cols(n)], op=ALU.subtract)
+
+        def v_qA(i):
+            quant(aq[:, i], asc[:, i], aT[i][:].rearrange("p k r t -> p (k r t)"), E5M2X4)
+
+        def v_mz(i):
+            V.tensor_scalar(out=gm[i][:], in0=gm[i][:], scalar1=EDGE, scalar2=None, op0=ALU.is_lt)
+
+        def v_gm(i):
+            V.tensor_tensor(out=gm[i][:], in0=gm[i][:], in1=gg[i][:], op=ALU.mult)
+            words(("g", i), gm[i][:])
+
+        def v_ht(i):
+            htp[i] = f4k([P, KP, PACK, P], "ht", 1)
+            V.tensor_scalar(out=htp[i][:].rearrange("p k t m -> p k m t"), in0=by_slot(ah[i][:]), scalar1=-1.0, scalar2=1.0, op0=ALU.max, op1=ALU.min)
+            for kp in range(KP):
+                e_ps[i, kp] = bank("ed", 2)
+                for t in range(PACK):
+                    for src, first in ((htp, True), (nhp, False)):
+                        PE.matmul(out=e_ps[i, kp][:, t * P:(t + 1) * P], lhsT=src[i][:, kp, t, :], rhs=ident[:], start=first, stop=not first, is_transpose=True)
+
+        def v_B(i):
+            bT[i] = sb([P, KP, P, PACK], BF16, "Tb", 1)
+            for kp in range(KP):
+                V.scalar_tensor_tensor(out=bT[i][:, kp], in0=e_ps[i, kp][:].rearrange("p (t r) -> p r t", t=PACK), scalar=-SIXTH, in1=gT[i][:, kp], op0=ALU.mult, op1=ALU.mult)
+
+        def v_qB(i):
+            quant(bq[:, i], bsc[:, i], bT[i][:].rearrange("p k r t -> p (k r t)"), E5M2X4)
+
+        def s_r(j):
+            hm[j] = b2k([P, 2, NB])
+            S.activation(out=hm[j][:], in_=arh[j][:], func=ACT.Square, scale=ROOT_3)
+            S.activation(out=arh[j][:], in_=arh[j][:], func=ACT.Relu, bias=half[:], scale=SIXTH)
+
+        def v_hm(j):
+            q, n = j % 4, j // 4
+            g, t = q // 2, 2 * (q % 2)
+            V.tensor_tensor(out=hm[j][:], in0=hm[j][:], in1=hg[g][:, t:t + 2, cols(n)], op=ALU.mult)
+
+        def v_mr(j):
+            V.tensor_scalar(out=hm[j][:], in0=hm[j][:], scalar1=EDGE, scalar2=None, op0=ALU.is_lt)
+
+        def pe_d(j):
+            q, n = j % 4, j // 4
+            for s in range(2):
+                i = 2 * q + s
+                d_ps[j, s] = bank("ed", 2)
+                for kp in range(KP):
+                    PE.matmul_mx(
+                        out=d_ps[j, s][:],
+                        lhsT=aq[:, i, kp * P:(kp + 1) * P].bitcast(E5M2X4),
+                        lhsT_scale=asc[:, i, kp * P:(kp + 1) * P],
+                        rhs=wq["h"][0][:, kp, cols(n)].bitcast(E4M3X4),
+                        rhs_scale=wq["h"][1][:, kp, cols(n)],
+                        start=kp == 0, stop=kp == KP - 1,
+                    )
+
+        def v_ED(j):
+            q, n = j % 4, j // 4
+            g, t = q // 2, 2 * (q % 2)
+            if t == 0:
+                dn[g, n] = sb([P, PACK, NB], BF16, "dn", 2)
+            for s in range(2):
+                V.scalar_tensor_tensor(out=arh[j][:, s], in0=arh[j][:, s], scalar=1.0, in1=d_ps[j, s][:], op0=ALU.min, op1=ALU.mult)
+                x = ut[2 * q + s][:, cols(n)]
+                G.tensor_tensor(out=x, in0=arh[j][:, s], in1=x, op=ALU.add)
+            key = ("d", j)
+            tr[key] = psum.tile([P, KP * 2, P], F32, name="tr", tag="tr", bufs=2)
+            for s in range(2):
+                V.scalar_tensor_tensor(out=dn[g, n][:, t + s], in0=d_ps[j, s][:], scalar=SIXTH, in1=hm[j][:, s], op0=ALU.mult, op1=ALU.mult)
+                w = dn[g, n][:, t + s].bitcast(F32)
+                for u in range(2):
+                    PE.transpose(tr[key][:, 2 * s + u, :], w[:, u:256:2], ident[:])
+
+        def s_cD(j):
+            dT[j] = s_words(("d", j))
+
+        def v_qD(j):
+            q, n = j % 4, j // 4
+            quant(fq[n][:, 2 * q:2 * q + 2].rearrange("p i r -> p (i r)"), fsc[n][:, 2 * q:2 * q + 2].rearrange("p i r -> p (i r)"), dT[j][:].rearrange("p k r t -> p (k r t)"), E5M2X4)
+
+        def pe_out0(i):
+            for n in range(2):
+                o_ps[i, n] = bank("oo", 4)
+                for k in range(2 * KP):
+                    kp = k % KP
+                    if k < KP:
+                        codes, scales = bq[:, i, kp * P:(kp + 1) * P], bsc[:, i, kp * P:(kp + 1) * P]
+                    else:
+                        codes, scales = fq[kp][:, i], fsc[kp][:, i]
+                    wc, ws = wq["z" if k < KP else "r"]
+                    PE.matmul_mx(
+                        out=o_ps[i, n][:], lhsT=codes.bitcast(E5M2X4), lhsT_scale=scales,
+                        rhs=wc[:, kp, cols(n)].bitcast(E4M3X4), rhs_scale=ws[:, kp, cols(n)],
+                        start=k == 0, stop=k == 2 * KP - 1,
+                    )
+
+        def v_out(i):
+            for n in range(2):
+                x = ut[i][:, cols(n)]
+                V.tensor_tensor(out=x, in0=o_ps[i, n][:], in1=x, op=ALU.add)
+            Q.dma_start(out=o0_h[:, i // 4, i % 4, :], in_=ut[i][:])
+
+        o1 = {}
+
+        def out1(b, eng):
+            m, n = b // 3, b % 3
+            acc = bank("oo", 4)
+            for g in range(KP):
+                PE.matmul_mx(
+                    out=acc[:],
+                    lhsT=dq[:, g, m * P:(m + 1) * P].bitcast(E5M2X4), lhsT_scale=dsc[:, g, m * P:(m + 1) * P],
+                    rhs=iq[:, g, cols(n)].bitcast(E4M3X4), rhs_scale=isc[:, g, cols(n)],
+                    start=g == 0, stop=g == KP - 1,
+                )
+            if b % 2 == 0:
+                o1[b // 2] = f4k([P, 2, NB], *(("az", AZB), ("nh", 1), ("az", AZB), ("ht", 1))[b // 2 % 4])
+            dst = o1[b // 2][:, b % 2, :]
+            if eng is S:
+                S.copy(out=dst, in_=acc[:])
+            else:
+                V.tensor_copy(out=dst, in_=acc[:])
+            Q.dma_start(out=out_1[m * P:(m + 1) * P, cols(n)], in_=dst)
+
+        def new_gr(key):
+            gr[key] = sb([P, H, PACK], BF16, "gr", 2)
+
+        def il(eng, key, src, c0, c1, off=0):
+            dst = gr[key][:, off + c0:off + c1, :].rearrange("p (c i) t -> p c t i", i=4)
+            s = src[:, :, c0:c1].rearrange("p t (c i) -> p c t i", i=4)
+            if eng is S:
+                S.copy(out=dst, in_=s)
+            else:
+                V.tensor_copy(out=dst, in_=s)
+
+        def q_cols(key, codes, scales, c0, c1, fmt):
+            quant(codes, scales, gr[key][:, c0:c1, :].rearrange("p c t -> p (c t)"), fmt)
+
+        def fill(eng, what):
+            kind = what[0]
+            if kind == "new":
+                new_gr(what[1])
+            elif kind == "il":
+                key, c0, c1 = what[1:]
+                if key in ("h0", "h1"):
+                    src = hg[int(key[1])]
+                elif key[0] == "d":
+                    src = dn[key[1], key[2]]
+                else:
+                    src = raw[key]
+                il(eng, key, src, c0, c1)
+            elif kind == "ilin":
+                g, c0, c1 = what[1:]
+                il(eng, "in", raw["in"][:, g], c0, c1, g * I)
+            elif kind == "qw":
+                n, kp = what[1]
+                c0, c1 = what[2:] if len(what) > 2 else (0, H)
+                q_cols((n, kp), wq[n][0][:, kp, c0:c1], wq[n][1][:, kp, c0:c1], c0, c1, E4M3X4)
+            elif kind == "qin":
+                g = what[1]
+                q_cols("in", iq[:, g, 0:I], isc[:, g, 0:I], g * I, (g + 1) * I, E4M3X4)
+            elif kind == "qh":
+                g, c0, c1 = what[1:]
+                q_cols("h%d" % g, iq[:, g, I + c0:I + c1], isc[:, g, I + c0:I + c1], c0, c1, E4M3X4)
+            elif kind == "qd":
+                g, n, c0, c1 = what[1:]
+                q_cols(("d", g, n), dq[:, g, n * NB + c0:n * NB + c1], dsc[:, g, n * NB + c0:n * NB + c1], c0, c1, E5M2X4)
+            elif kind == "x":
+                for b in range(what[1], what[2]):
+                    out1(b, eng)
+            elif kind == "out0":
+                pe_out0(what[1])
+            elif kind == "out":
+                v_out(what[1])
+            elif kind == "load":
+                (load_in if what[1] == "in" else lambda: load_w(*what[1]))()
+
+        def fills(eng, table, *key):
+            for w in table.get(key, []):
+                fill(eng, w)
+
+        load_az(0)
+        load_g(0)
+        load_ah(0)
+        load_h(0)
+        load_w("h", 0)
+        load_az(1)
+        load_g(1)
+        load_ah(1)
+        load_h(1)
+        s_p(0)
+        s_qh(0)
+        s_qz(0)
+        s_nh(0)
+        for k in range(TILES + 1):
+            a = k if k < TILES else None
+            m = k - 1 if k > 0 else None
+            n = k + 1 if k + 1 < TILES else None
+            if k + 2 < TILES:
+                load_az(k + 2)
+                load_g(k + 2)
+                load_ah(k + 2)
+                load_h(k + 2)
+            fills(Q, LOADS, k)
+            if a is not None:
+                v_u(a)
+                v_A(a)
+                gz(G, a, 0)
+            if n is not None:
+                s_p(n)
+                s_qh(n)
+            if m is not None:
+                v_B(m)
+                v_qA(m)
+            if a is not None:
+                gz(V, a, 1)
+                aT[a] = s_words(("a", a))
+            if n is not None:
+                s_qz(n)
+            fills(S, S1, k, 0)
+            if a is not None:
+                v_mz(a)
+                v_ht(a)
+                v_gm(a)
+            if m is not None:
+                v_qB(m)
+            if n is not None:
+                s_nh(n)
+            fills(S, S1, k, 1)
+            fills(V, V1, k, 0)
+            if a is not None:
+                gT[a] = s_words(("g", a))
+            fills(V, V1, k, 1)
+
+        for j in range(9):
+            if j + 2 < 8 and j > 0:
+                load_ar(j + 2)
+            fills(Q, LOADS, "u", j)
+            if j == 0:
+                for x in range(3):
+                    load_ar(x)
+                s_r(0)
+                pe_d(0)
+                v_mr(0)
+                v_hm(0)
+            if j < 8:
+                v_ED(j)
+            if j + 1 < 8:
+                pe_d(j + 1)
+                s_r(j + 1)
+            fills(S, S2, j, 0)
+            fills(V, V2, j, 0)
+            if j > 0:
+                v_qD(j - 1)
+            if j < 8:
+                s_cD(j)
+            if j + 1 < 8:
+                v_mr(j + 1)
+            fills(V, V2, j, 1)
+            if j + 1 < 8:
+                v_hm(j + 1)
+            fills(S, S2, j, 1)
+            fills(V, V2, j, 2)
+            fills(S, S2, j, 2)

@@ -21,69 +21,14 @@ BYTES = 2 * (B * I + B * H + 3 * H * H + B * H) + 4 * 3 * B * H + 4 * (B * H + H
 P = 128
 PACK = 4
 NB = 512
-TILES = 8
 KP = 2
+TILES = 8
+PAIR = 2 * P
 
 SIXTH = 1.0 / 6.0
 EDGE = 1.0 + 2.0 ** -8
 ROOT_1 = math.sqrt(EDGE) * (1.0 + 2.0 ** -22)
 ROOT_3 = ROOT_1 / 3.0
-
-AZB, B2K = 3, 6
-
-
-def il_cut(key, c0, c1, step=256):
-    return [("il", key, c, min(c + step, c1)) for c in range(c0, c1, step)]
-
-
-def in_cut(g):
-    return [("ilin", g, c, c + 256) for c in (0, 256)]
-
-
-LOADS = {(1,): [("load", ("h", 1))], (4,): [("load", "in")], (5,): [("load", ("z", 0))], (7,): [("load", ("z", 1))], ("u", 1): [("load", ("r", 0))], ("u", 3): [("load", ("r", 1))]}
-V1 = {
-    (0, 0): [("new", ("h", 0))] + il_cut(("h", 0), 0, 512, 512),
-    (0, 1): il_cut(("h", 0), 512, 1024, 512),
-    (1, 0): [("qw", ("h", 0))],
-    (2, 0): [("new", ("h", 1))] + il_cut(("h", 1), 0, 512, 512),
-    (3, 0): il_cut(("h", 1), 512, 1024, 512), (4, 0): [("qw", ("h", 1))],
-    (6, 0): [("qin", 0), ("qin", 1)],
-    (7, 1): [("qh", 0, 0, 1024)],
-    (8, 1): [("new", ("z", 0))] + il_cut(("z", 0), 0, 1024, 512),
-}
-S1 = {
-    (5, 0): [("new", "in")] + in_cut(0), (5, 1): in_cut(1),
-    (6, 0): [("new", "h0")] + il_cut("h0", 0, 256), (6, 1): il_cut("h0", 256, 512),
-    (7, 0): il_cut("h0", 512, 1024),
-    (8, 0): [("new", "h1")] + il_cut("h1", 0, 512),
-}
-V2 = {
-    (0, 2): [("qw", ("z", 0)), ("qh", 1, 0, 1024)],
-    (2, 2): [("new", ("z", 1))] + il_cut(("z", 1), 0, 1024, 512) + [("qw", ("z", 1)), ("qd", 0, 0, 0, 512)],
-    (4, 0): il_cut(("d", 1, 0), 0, 256),
-    (4, 2): [("qd", 1, 0, 0, 256), ("qd", 1, 0, 256, 512)],
-    (4, 1): [("qw", ("r", 0))],
-    (5, 2): [("qw", ("r", 1)), ("out0", 0), ("out0", 1)],
-    (6, 0): [("out", 0), ("out", 1)],
-    (6, 2): [("out0", 2), ("out0", 3)],
-    (7, 0): [("out", 2), ("out", 3)],
-    (7, 2): [("qd", 0, 1, 0, 512), ("out0", 4), ("out0", 5)],
-    (8, 0): il_cut(("d", 1, 1), 0, 256) + [("out", 4), ("out", 5), ("qd", 1, 1, 0, 256)],
-    (8, 2): [("qd", 1, 1, 256, 512), ("out0", 6), ("out", 6), ("out0", 7), ("out", 7)],
-}
-S2 = {
-    (0, 0): il_cut("h1", 512, 1024),
-    (2, 1): [("new", ("d", 0, 0))] + il_cut(("d", 0, 0), 0, 512),
-    (3, 0): [("new", ("r", 0))] + il_cut(("r", 0), 0, 512), (3, 1): il_cut(("r", 0), 512, 1024),
-    (4, 0): [("new", ("d", 1, 0))] + il_cut(("d", 1, 0), 256, 512),
-    (4, 1): [("new", ("r", 1))] + il_cut(("r", 1), 0, 512),
-    (5, 0): il_cut(("r", 1), 512, 1024),
-    (5, 1): [("x", 0, 4)],
-    (6, 0): [("new", ("d", 0, 1))] + il_cut(("d", 0, 1), 0, 256), (6, 1): il_cut(("d", 0, 1), 256, 512) + [("x", 4, 8)],
-    (7, 1): [("x", 8, 12)],
-    (8, 0): [("new", ("d", 1, 1))] + il_cut(("d", 1, 1), 256, 512),
-    (8, 2): [("x", 12, 24)],
-}
 
 
 def tile_grucell_v_kernel(
@@ -102,374 +47,574 @@ def tile_grucell_v_kernel(
     with ExitStack() as ctx:
         pool = ctx.enter_context(tc.tile_pool(name="sb", bufs=1))
         psum = ctx.enter_context(tc.psum_pool(name="ps", bufs=1))
+        ctx.enter_context(tc.manual_schedule())
 
         def sb(shape, dt, tag, bufs=1):
             return pool.tile(shape, dt, name=tag, tag=tag, bufs=bufs, align_bytes=64)
 
-        def f4k(shape, tag, bufs):
-            return sb(shape, F32, tag, bufs)
+        def bank(n):
+            return psum.tile([P, NB], F32, name="bank%d" % n, tag="bank%d" % n, bufs=1)
 
-        def b2k(shape):
-            return sb(shape, BF16, "b2k", B2K)
-
-        def bank(tag, bufs):
-            return psum.tile([P, NB], F32, name=tag, tag=tag, bufs=bufs)
+        def cols(n, width=NB):
+            return slice(n * width, (n + 1) * width)
 
         half = sb([P, 1], F32, "half")
         ident = sb([P, P], F32, "ident")
-        V.memset(half[:], 0.5)
-        make_identity(nc, ident[:])
 
-        wq = {n: (sb([P, KP, H], U32, "wq" + n), sb([P, KP, H], U8, "ws" + n)) for n in "hzr"}
-        iq, isc = sb([P, KP, C], U32, "iq"), sb([P, KP, C], U8, "isc")
-        dq, dsc = sb([P, KP, H], U32, "dq"), sb([P, KP, H], U8, "dsc")
-        aq, asc = sb([P, TILES, KP * P], U32, "aq"), sb([P, TILES, KP * P], U8, "asc")
-        bq, bsc = sb([P, TILES, KP * P], U32, "bq"), sb([P, TILES, KP * P], U8, "bsc")
-        fq = [sb([P, TILES, P], U32, "fq%d" % n) for n in range(KP)]
-        fsc = [sb([P, TILES, P], U8, "fsc%d" % n) for n in range(KP)]
-        hg = [sb([P, PACK, H], BF16, "hg%d" % g) for g in range(KP)]
-        ut = [sb([P, H], F32, "u%d" % i) for i in range(TILES)]
+        w_scales = {n: sb([P, KP, H], U8, "ws" + n) for n in "hzr"}
+        w_codes = {n: sb([P, KP, H], U32, "wc" + n) for n in "hz"}
+        ih_codes, ih_scales = sb([P, KP, C], U32, "ihc"), sb([P, KP, C], U8, "ihs")
+        dz2_codes, dz2_scales = sb([P, TILES, KP * P], U32, "dz2c"), sb([P, TILES, KP * P], U8, "dz2s")
+        daz_codes, daz_scales = sb([P, TILES, KP * P], U32, "dazc"), sb([P, TILES, KP * P], U8, "dazs")
+        dar_scales = [sb([P, 2, H], U8, "dars%d" % g) for g in range(KP)]
+        dar_codes = {0: sb([P, 2, H], U32, "darc0")}
+        terms = [sb([P, PACK, H], F32, "terms%d" % g) for g in range(KP)]
 
-        az, ah, gg, raw, gr = {}, {}, {}, {}, {}
-        qh, gm, ab, aT, gT, bT, dT = {}, {}, {}, {}, {}, {}, {}
-        htp, nhp, e_ps, tr = {}, {}, {}, {}
-        arh, hm, dn, d_ps, o_ps = {}, {}, {}, {}, {}
+        az, ah, gg, raw, h_nat, h_il, grouped = {}, {}, {}, {}, {}, {}, {}
+        qh, qz, clip, neg_h, e_ps, dz2_t, gm_t, daz_t, words_ps = {}, {}, {}, {}, {}, {}, {}, {}, {}
+        ar, hm, d_ps, turn_ps, dar_t, o_ps = {}, {}, {}, {}, {}, {}
+
+        def load_az(i):
+            az[i] = sb([P, H], F32, "az", 2)
+            Q.dma_start(out=az[i][:], in_=az_h[:, i // 4, i % 4, :])
+
+        def load_ah(i):
+            ah[i] = sb([P, H], F32, "ah", 2)
+            Q.dma_start(out=ah[i][:], in_=ah_h[:, i // 4, i % 4, :])
+
+        def load_g(i):
+            gg[i] = sb([P, H], BF16, "gg", 4)
+            Q.dma_start(out=gg[i][:], in_=g_h[:, i // 4, i % 4, :])
+
+        def load_h(g, t0, t1):
+            if t0 == 0:
+                h_nat[g] = sb([P, PACK, H], BF16, ("wcr", "darc1")[g])
+            Q.dma_start(out=h_nat[g][:, t0:t1, :], in_=h_h[:, g, t0:t1, :])
 
         def load_w(n, kp):
             raw[n, kp] = sb([P, PACK, H], BF16, "raw", 2)
             Q.dma_start(out=raw[n, kp][:], in_=w_h[n][:, kp])
 
-        def load_in():
+        def load_inputs():
             raw["in"] = sb([P, KP, PACK, I], BF16, "raw", 2)
             Q.dma_start(out=raw["in"][:], in_=in_h)
 
-        def load_az(i):
-            az[i] = f4k([P, H], "az", AZB)
-            Q.dma_start(out=az[i][:], in_=az_h[:, i // 4, i % 4, :])
-
-        def load_ah(i):
-            ah[i] = f4k([P, H], "ah", 3)
-            Q.dma_start(out=ah[i][:], in_=ah_h[:, i // 4, i % 4, :])
-
-        def load_g(i):
-            gg[i] = sb([P, H], BF16, "gg", 3)
-            Q.dma_start(out=gg[i][:], in_=g_h[:, i // 4, i % 4, :])
-
-        def load_h(i):
-            Q.dma_start(out=hg[i // 4][:, i % 4, :], in_=h_h[:, i // 4, i % 4, :])
-
-        def load_ar(j):
-            q, n = j % 4, j // 4
-            g, t = q // 2, 2 * (q % 2)
-            arh[j] = f4k([P, 2, NB], "ah", 3)
-            Q.dma_start(out=arh[j][:], in_=ar_h[:, g, t:t + 2, n * NB:(n + 1) * NB])
-
-        def cols(n):
-            return slice(n * NB, (n + 1) * NB)
-
-        def s_p(i):
-            S.activation(out=ut[i][:], in_=az[i][:], func=ACT.Relu, bias=half[:], scale=-SIXTH)
-
-        def s_qh(i):
-            qh[i] = b2k([P, H])
-            S.activation(out=qh[i][:], in_=ah[i][:], func=ACT.Square, scale=ROOT_1)
-
-        def s_qz(i):
-            gm[i] = b2k([P, H])
-            S.activation(out=gm[i][:], in_=az[i][:], func=ACT.Square, scale=ROOT_3)
-
-        def by_slot(x):
-            return x.rearrange("p (k m t) -> p k m t", k=KP, t=PACK)
-
-        def s_nh(i):
-            nhp[i] = f4k([P, KP, PACK, P], "nh", 1)
-            S.activation(out=nhp[i][:].rearrange("p k t m -> p k m t"), in_=by_slot(hg[i // 4][:, i % 4, :]), func=ACT.Copy, scale=-1.0)
-
-        def words(key, src):
-            tr[key] = psum.tile([P, KP * 2, P], F32, name="tr", tag="tr", bufs=2)
-            w = src.bitcast(F32)
-            for kp in range(KP):
-                for u in range(2):
-                    PE.transpose(tr[key][:, 2 * kp + u, :], w[:, 256 * kp + u:256 * (kp + 1):2], ident[:])
-
-        def s_words(key):
-            out = sb([P, KP, P, PACK], BF16, "T" + key[0], 1)
-            S.copy(out=out[:].bitcast(F32), in_=tr[key][:].rearrange("p (k u) r -> p k r u", k=KP))
-            return out
+        def load_ar(x):
+            ar[x] = sb([P, PACK, NB], F32, "ar", 2)
+            Q.dma_start(out=ar[x][:], in_=ar_h[:, x // KP, :, cols(x % KP)])
 
         def quant(codes, scales, src, fmt):
             V.quantize_mx(out=codes.bitcast(fmt), scales=scales, in_=src)
 
+        def interleave(eng, dst, src):
+            dst = dst.rearrange("p (c i t) -> p c t i", i=4, t=PACK)
+            src = src.rearrange("p t (c i) -> p c t i", i=4)
+            if eng is S:
+                S.copy(out=dst, in_=src)
+            else:
+                V.tensor_copy(out=dst, in_=src)
+
+        def il(eng, key):
+            if key[0] == "hp":
+                g, n = key[1:]
+                if n == 0:
+                    h_il[g] = sb([P, H * PACK], BF16, "hil")
+                interleave(eng, h_il[g][:, cols(n, NB * PACK)], h_nat[g][:, :, cols(n)])
+                return
+            grouped[key] = sb([P, NB * PACK], BF16, "grouped", 2)
+            src = raw["in"][:, key[1]] if key[0] == "in" else raw[key[0], key[1]][:, :, cols(key[2])]
+            interleave(eng, grouped[key][:], src)
+
+        def qe(key):
+            if key[0] == "hp":
+                g, n = key[1:]
+                at = slice(I + n * NB, I + (n + 1) * NB)
+                quant(ih_codes[:, g, at], ih_scales[:, g, at], h_il[g][:, cols(n, NB * PACK)], E4M3X4)
+            elif key[0] == "in":
+                quant(ih_codes[:, key[1], 0:I], ih_scales[:, key[1], 0:I], grouped[key][:], E4M3X4)
+            else:
+                n, kp, x = key
+                if n not in w_codes:
+                    w_codes[n] = sb([P, KP, H], U32, "wc" + n)
+                quant(w_codes[n][:, kp, cols(x)], w_scales[n][:, kp, cols(x)], grouped[key][:], E4M3X4)
+
+        def term(i):
+            return terms[i // 4][:, i % 4, :]
+
+        def s_p(i):
+            S.activation(out=term(i), in_=az[i][:], func=ACT.Relu, bias=half[:], scale=-SIXTH)
+
+        def s_qh(i):
+            qh[i] = sb([P, H], BF16, "qh", 2)
+            S.activation(out=qh[i][:], in_=ah[i][:], func=ACT.Square, scale=ROOT_1)
+
+        def s_qz(i):
+            qz[i] = sb([P, H], BF16, "qz", 2)
+            S.activation(out=qz[i][:], in_=az[i][:], func=ACT.Square, scale=ROOT_3)
+
+        def negate_h(eng, i):
+            neg_h[i] = sb([P, PACK, KP * P], F32, "negh", 2)
+            dst = neg_h[i][:].rearrange("p s (b e) -> p b s e", e=4)
+            src = h_nat[i // 4][:, i % 4, :].rearrange("p (b e s) -> p b s e", e=4, s=PACK)
+            if eng is S:
+                S.activation(out=dst, in_=src, func=ACT.Copy, scale=-1.0)
+            else:
+                V.tensor_scalar(out=dst, in0=src, scalar1=-1.0, scalar2=None, op0=ALU.mult)
+
+        def v_clip(i):
+            clip[i] = sb([P, PACK, KP * P], F32, "clip")
+            V.tensor_scalar(out=clip[i][:].rearrange("p s n -> p n s"), in0=ah[i][:].rearrange("p (n s) -> p n s", s=PACK),
+                            scalar1=-1.0, scalar2=1.0, op0=ALU.max, op1=ALU.min)
+
+        def pe_e(i):
+            for kp in range(KP):
+                e_ps[i, kp] = bank(2 * (i % 2) + kp)
+                for s in range(PACK):
+                    for src, first in ((clip, True), (neg_h, False)):
+                        PE.matmul(out=e_ps[i, kp][:, cols(s, P)], lhsT=src[i][:, s, cols(kp, P)], rhs=ident[:],
+                                  start=first, stop=not first, is_transpose=True)
+
+        def turn_words(key, src, n):
+            words_ps[key] = bank(n)
+            w = src.bitcast(F32)
+            for kp in range(KP):
+                for u in range(2):
+                    PE.transpose(words_ps[key][:, cols(2 * kp + u, P)], w[:, 256 * kp + u:256 * (kp + 1):2], ident[:])
+
+        def s_words(key):
+            out = sb([P, KP, P, PACK], BF16, "turned" + key[0], 2)
+            S.copy(out=out[:].bitcast(F32), in_=words_ps[key][:].rearrange("p (k u r) -> p k r u", k=KP, u=2))
+            return out
+
         def v_u(i):
-            V.scalar_tensor_tensor(out=ut[i][:], in0=ut[i][:], scalar=1.0, in1=gg[i][:], op0=ALU.min, op1=ALU.mult)
+            V.scalar_tensor_tensor(out=term(i), in0=term(i), scalar=1.0, in1=gg[i][:], op0=ALU.min, op1=ALU.mult)
 
-        def v_A(i):
-            a = b2k([P, H])
-            V.scalar_tensor_tensor(out=a[:], in0=qh[i][:], scalar=EDGE, in1=ut[i][:], op0=ALU.is_lt, op1=ALU.mult)
-            words(("a", i), a[:])
-
-        def gz(eng, i, n):
-            eng.tensor_tensor(out=ut[i][:, cols(n)], in0=gg[i][:, cols(n)], in1=ut[i][:, cols(n)], op=ALU.subtract)
-
-        def v_qA(i):
-            quant(aq[:, i], asc[:, i], aT[i][:].rearrange("p k r t -> p (k r t)"), E5M2X4)
+        def v_dz2(i):
+            V.scalar_tensor_tensor(out=qh[i][:], in0=qh[i][:], scalar=EDGE, in1=term(i), op0=ALU.is_lt, op1=ALU.mult)
+            turn_words(("a", i), qh[i][:], 4)
 
         def v_mz(i):
-            V.tensor_scalar(out=gm[i][:], in0=gm[i][:], scalar1=EDGE, scalar2=None, op0=ALU.is_lt)
+            V.tensor_scalar(out=qz[i][:], in0=qz[i][:], scalar1=EDGE, scalar2=None, op0=ALU.is_lt)
 
         def v_gm(i):
-            V.tensor_tensor(out=gm[i][:], in0=gm[i][:], in1=gg[i][:], op=ALU.mult)
-            words(("g", i), gm[i][:])
+            V.tensor_tensor(out=qz[i][:], in0=qz[i][:], in1=gg[i][:], op=ALU.mult)
+            turn_words(("g", i), qz[i][:], 5)
 
-        def v_ht(i):
-            htp[i] = f4k([P, KP, PACK, P], "ht", 1)
-            V.tensor_scalar(out=htp[i][:].rearrange("p k t m -> p k m t"), in0=by_slot(ah[i][:]), scalar1=-1.0, scalar2=1.0, op0=ALU.max, op1=ALU.min)
-            for kp in range(KP):
-                e_ps[i, kp] = bank("ed", 2)
-                for t in range(PACK):
-                    for src, first in ((htp, True), (nhp, False)):
-                        PE.matmul(out=e_ps[i, kp][:, t * P:(t + 1) * P], lhsT=src[i][:, kp, t, :], rhs=ident[:], start=first, stop=not first, is_transpose=True)
+        def less_g(eng, i, at=slice(0, H)):
+            y = term(i)[:, at]
+            eng.tensor_tensor(out=y, in0=y, in1=gg[i][:, at], op=ALU.subtract)
 
-        def v_B(i):
-            bT[i] = sb([P, KP, P, PACK], BF16, "Tb", 1)
-            for kp in range(KP):
-                V.scalar_tensor_tensor(out=bT[i][:, kp], in0=e_ps[i, kp][:].rearrange("p (t r) -> p r t", t=PACK), scalar=-SIXTH, in1=gT[i][:, kp], op0=ALU.mult, op1=ALU.mult)
+        def plus_g(i, n):
+            y = term(i)[:, cols(n)]
+            V.tensor_tensor(out=y, in0=y, in1=gg[i][:, cols(n)], op=ALU.add)
 
-        def v_qB(i):
-            quant(bq[:, i], bsc[:, i], bT[i][:].rearrange("p k r t -> p (k r t)"), E5M2X4)
+        def v_daz(i, kp):
+            if kp == 0:
+                daz_t[i] = sb([P, KP, P, PACK], BF16, "daz")
+            V.scalar_tensor_tensor(out=daz_t[i][:, kp], in0=e_ps[i, kp][:].rearrange("p (s r) -> p r s", s=PACK),
+                                   scalar=-SIXTH, in1=gm_t[i][:, kp], op0=ALU.mult, op1=ALU.mult)
+
+        def q_dz2(i):
+            quant(dz2_codes[:, i], dz2_scales[:, i], dz2_t[i][:].rearrange("p k r s -> p (k r s)"), E5M2X4)
+
+        def q_daz(i):
+            quant(daz_codes[:, i], daz_scales[:, i], daz_t[i][:].rearrange("p k r s -> p (k r s)"), E5M2X4)
+
+        def s_qr(j):
+            x, at = j // 2, cols(j % 2, PAIR)
+            if j % 2 == 0:
+                hm[x] = sb([P, NB * PACK], BF16, "hm", 2)
+            S.activation(out=hm[x][:, cols(j % 2, PAIR * PACK)].rearrange("p (c i t) -> p c t i", i=4, t=PACK),
+                         in_=ar[x][:, :, at].rearrange("p t (c i) -> p c t i", i=4), func=ACT.Square, scale=ROOT_3)
 
         def s_r(j):
-            hm[j] = b2k([P, 2, NB])
-            S.activation(out=hm[j][:], in_=arh[j][:], func=ACT.Square, scale=ROOT_3)
-            S.activation(out=arh[j][:], in_=arh[j][:], func=ACT.Relu, bias=half[:], scale=SIXTH)
-
-        def v_hm(j):
-            q, n = j % 4, j // 4
-            g, t = q // 2, 2 * (q % 2)
-            V.tensor_tensor(out=hm[j][:], in0=hm[j][:], in1=hg[g][:, t:t + 2, cols(n)], op=ALU.mult)
+            x, at = j // 2, cols(j % 2, PAIR)
+            S.activation(out=ar[x][:, :, at], in_=ar[x][:, :, at], func=ACT.Relu, bias=half[:], scale=SIXTH)
 
         def v_mr(j):
-            V.tensor_scalar(out=hm[j][:], in0=hm[j][:], scalar1=EDGE, scalar2=None, op0=ALU.is_lt)
+            y = hm[j // 2][:, cols(j % 2, PAIR * PACK)]
+            V.tensor_scalar(out=y, in0=y, scalar1=EDGE, scalar2=None, op0=ALU.is_lt)
+
+        def v_hm(j):
+            y = hm[j // 2][:, cols(j % 2, PAIR * PACK)]
+            V.tensor_tensor(out=y, in0=y, in1=h_il[j // 4][:, cols(j % 4, PAIR * PACK)], op=ALU.mult)
 
         def pe_d(j):
-            q, n = j % 4, j // 4
-            for s in range(2):
-                i = 2 * q + s
-                d_ps[j, s] = bank("ed", 2)
-                for kp in range(KP):
-                    PE.matmul_mx(
-                        out=d_ps[j, s][:],
-                        lhsT=aq[:, i, kp * P:(kp + 1) * P].bitcast(E5M2X4),
-                        lhsT_scale=asc[:, i, kp * P:(kp + 1) * P],
-                        rhs=wq["h"][0][:, kp, cols(n)].bitcast(E4M3X4),
-                        rhs_scale=wq["h"][1][:, kp, cols(n)],
-                        start=kp == 0, stop=kp == KP - 1,
-                    )
+            for b in range(2):
+                d_ps[j, b] = bank(6 + b)
+                at = cols(2 * (j % 4) + b, P)
+                for t in range(PACK):
+                    i = PACK * (j // 4) + t
+                    for kp in range(KP):
+                        PE.matmul_mx(
+                            out=d_ps[j, b][:, cols(t, P)],
+                            lhsT=dz2_codes[:, i, cols(kp, P)].bitcast(E5M2X4), lhsT_scale=dz2_scales[:, i, cols(kp, P)],
+                            rhs=w_codes["h"][:, kp, at].bitcast(E4M3X4), rhs_scale=w_scales["h"][:, kp, at],
+                            start=kp == 0, stop=kp == KP - 1,
+                        )
 
-        def v_ED(j):
-            q, n = j % 4, j // 4
-            g, t = q // 2, 2 * (q % 2)
-            if t == 0:
-                dn[g, n] = sb([P, PACK, NB], BF16, "dn", 2)
-            for s in range(2):
-                V.scalar_tensor_tensor(out=arh[j][:, s], in0=arh[j][:, s], scalar=1.0, in1=d_ps[j, s][:], op0=ALU.min, op1=ALU.mult)
-                x = ut[2 * q + s][:, cols(n)]
-                G.tensor_tensor(out=x, in0=arh[j][:, s], in1=x, op=ALU.add)
-            key = ("d", j)
-            tr[key] = psum.tile([P, KP * 2, P], F32, name="tr", tag="tr", bufs=2)
-            for s in range(2):
-                V.scalar_tensor_tensor(out=dn[g, n][:, t + s], in0=d_ps[j, s][:], scalar=SIXTH, in1=hm[j][:, s], op0=ALU.mult, op1=ALU.mult)
-                w = dn[g, n][:, t + s].bitcast(F32)
-                for u in range(2):
-                    PE.transpose(tr[key][:, 2 * s + u, :], w[:, u:256:2], ident[:])
+        def v_pair(j):
+            x = j // 2
+            for b in range(2):
+                r = ar[x][:, :, cols(2 * (j % 2) + b, P)]
+                V.scalar_tensor_tensor(out=r, in0=r, scalar=1.0, in1=d_ps[j, b][:].rearrange("p (t c) -> p t c", t=PACK),
+                                       op0=ALU.min, op1=ALU.mult)
+                y = terms[j // 4][:, :, cols(2 * (j % 4) + b, P)]
+                G.tensor_tensor(out=y, in0=r, in1=y, op=ALU.subtract)
+            for b in range(2):
+                y = hm[x][:, cols(2 * (j % 2) + b, NB)].rearrange("p (c t) -> p c t", t=PACK)
+                V.scalar_tensor_tensor(out=y, in0=d_ps[j, b][:].rearrange("p (t c) -> p c t", t=PACK), scalar=SIXTH, in1=y,
+                                       op0=ALU.mult, op1=ALU.mult)
 
-        def s_cD(j):
-            dT[j] = s_words(("d", j))
+        def q_tok(j):
+            g, at = j // 4, cols(j % 4, PAIR)
+            if g not in dar_codes:
+                dar_codes[g] = sb([P, 2, H], U32, "darc%d" % g)
+            quant(dar_codes[g][:, 0, at], dar_scales[g][:, 0, at], hm[j // 2][:, cols(j % 2, PAIR * PACK)], E5M2X4)
 
-        def v_qD(j):
-            q, n = j % 4, j // 4
-            quant(fq[n][:, 2 * q:2 * q + 2].rearrange("p i r -> p (i r)"), fsc[n][:, 2 * q:2 * q + 2].rearrange("p i r -> p (i r)"), dT[j][:].rearrange("p k r t -> p (k r t)"), E5M2X4)
+        def pe_turn(x):
+            w = hm[x][:].bitcast(F32)
+            for tp in range(2):
+                turn_ps[x, tp] = bank(4 + tp)
+                for s in range(PACK):
+                    PE.transpose(turn_ps[x, tp][:, cols(s, P)], w[:, 2 * s + tp::8], ident[:])
 
-        def pe_out0(i):
-            for n in range(2):
-                o_ps[i, n] = bank("oo", 4)
-                for k in range(2 * KP):
-                    kp = k % KP
-                    if k < KP:
-                        codes, scales = bq[:, i, kp * P:(kp + 1) * P], bsc[:, i, kp * P:(kp + 1) * P]
-                    else:
-                        codes, scales = fq[kp][:, i], fsc[kp][:, i]
-                    wc, ws = wq["z" if k < KP else "r"]
-                    PE.matmul_mx(
-                        out=o_ps[i, n][:], lhsT=codes.bitcast(E5M2X4), lhsT_scale=scales,
-                        rhs=wc[:, kp, cols(n)].bitcast(E4M3X4), rhs_scale=ws[:, kp, cols(n)],
-                        start=k == 0, stop=k == 2 * KP - 1,
-                    )
+        def s_turn(x, tp):
+            if tp == 0:
+                dar_t[x] = sb([P, 2, 2 * P * PACK], BF16, "dart")
+            S.copy(out=dar_t[x][:, tp].rearrange("p (e r s) -> p e r s", e=2, s=PACK),
+                   in_=turn_ps[x, tp][:].bitcast(BF16).rearrange("p (s r e) -> p e r s", s=PACK, e=2))
 
-        def v_out(i):
-            for n in range(2):
-                x = ut[i][:, cols(n)]
-                V.tensor_tensor(out=x, in0=o_ps[i, n][:], in1=x, op=ALU.add)
-            Q.dma_start(out=o0_h[:, i // 4, i % 4, :], in_=ut[i][:])
+        def q_feat(x, tp0=0, tp1=2):
+            g, at = x // KP, slice((x % KP) * NB + tp0 * PAIR, (x % KP) * NB + tp1 * PAIR)
+            quant(dar_codes[g][:, 1, at], dar_scales[g][:, 1, at], dar_t[x][:, tp0:tp1].rearrange("p a b -> p (a b)"), E5M2X4)
 
-        o1 = {}
+        def pe_out0(i, n, at_bank, passes=range(2 * KP)):
+            g, t = i // 4, i % 4
+            if passes[0] == 0:
+                o_ps[i, n] = bank(at_bank)
+            for k in passes:
+                kp = k % KP
+                if k < KP:
+                    codes, scales = daz_codes[:, i, cols(kp, P)], daz_scales[:, i, cols(kp, P)]
+                else:
+                    at = cols(PACK * kp + t, P)
+                    codes, scales = dar_codes[g][:, 1, at], dar_scales[g][:, 1, at]
+                gate = "z" if k < KP else "r"
+                PE.matmul_mx(
+                    out=o_ps[i, n][:], lhsT=codes.bitcast(E5M2X4), lhsT_scale=scales,
+                    rhs=w_codes[gate][:, kp, cols(n)].bitcast(E4M3X4), rhs_scale=w_scales[gate][:, kp, cols(n)],
+                    start=k == 0, stop=k == 2 * KP - 1,
+                )
 
-        def out1(b, eng):
-            m, n = b // 3, b % 3
-            acc = bank("oo", 4)
+        def v_out0(i, n):
+            y = terms[i // 4][:, i % 4, cols(n)]
+            V.tensor_tensor(out=y, in0=o_ps[i, n][:], in1=y, op=ALU.add)
+            Q.dma_start(out=o0_h[:, i // 4, i % 4, cols(n)], in_=y)
+
+        stage = {}
+
+        blocks = []
+        for j in range(4):
+            blocks.extend([(m, n) for m in (2 * j, 2 * j + 1) for n in range(1 if j < 2 else 0, 3)])
+            if j in (1, 2):
+                blocks.extend([(m, 0) for m in (2 * j - 2, 2 * j - 1)])
+
+        def pe_out1(b, at_bank=None):
+            m, n = blocks[b]
+            o_ps[b] = bank(b % 4 if at_bank is None else at_bank)
             for g in range(KP):
                 PE.matmul_mx(
-                    out=acc[:],
-                    lhsT=dq[:, g, m * P:(m + 1) * P].bitcast(E5M2X4), lhsT_scale=dsc[:, g, m * P:(m + 1) * P],
-                    rhs=iq[:, g, cols(n)].bitcast(E4M3X4), rhs_scale=isc[:, g, cols(n)],
+                    out=o_ps[b][:],
+                    lhsT=dar_codes[g][:, 0, cols(m, P)].bitcast(E5M2X4), lhsT_scale=dar_scales[g][:, 0, cols(m, P)],
+                    rhs=ih_codes[:, g, cols(n)].bitcast(E4M3X4), rhs_scale=ih_scales[:, g, cols(n)],
                     start=g == 0, stop=g == KP - 1,
                 )
+
+        def out1(eng, b):
+            m, n = blocks[b]
             if b % 2 == 0:
-                o1[b // 2] = f4k([P, 2, NB], *(("az", AZB), ("nh", 1), ("az", AZB), ("ht", 1))[b // 2 % 4])
-            dst = o1[b // 2][:, b % 2, :]
+                stage[b // 2] = sb([P, 2, NB], F32, ("az", "ah")[b // 2 % 2], 2)
+            dst = stage[b // 2][:, b % 2, :]
             if eng is S:
-                S.copy(out=dst, in_=acc[:])
+                S.copy(out=dst, in_=o_ps[b][:])
             else:
-                V.tensor_copy(out=dst, in_=acc[:])
-            Q.dma_start(out=out_1[m * P:(m + 1) * P, cols(n)], in_=dst)
-
-        def new_gr(key):
-            gr[key] = sb([P, H, PACK], BF16, "gr", 2)
-
-        def il(eng, key, src, c0, c1, off=0):
-            dst = gr[key][:, off + c0:off + c1, :].rearrange("p (c i) t -> p c t i", i=4)
-            s = src[:, :, c0:c1].rearrange("p t (c i) -> p c t i", i=4)
-            if eng is S:
-                S.copy(out=dst, in_=s)
-            else:
-                V.tensor_copy(out=dst, in_=s)
-
-        def q_cols(key, codes, scales, c0, c1, fmt):
-            quant(codes, scales, gr[key][:, c0:c1, :].rearrange("p c t -> p (c t)"), fmt)
-
-        def fill(eng, what):
-            kind = what[0]
-            if kind == "new":
-                new_gr(what[1])
-            elif kind == "il":
-                key, c0, c1 = what[1:]
-                if key in ("h0", "h1"):
-                    src = hg[int(key[1])]
-                elif key[0] == "d":
-                    src = dn[key[1], key[2]]
-                else:
-                    src = raw[key]
-                il(eng, key, src, c0, c1)
-            elif kind == "ilin":
-                g, c0, c1 = what[1:]
-                il(eng, "in", raw["in"][:, g], c0, c1, g * I)
-            elif kind == "qw":
-                n, kp = what[1]
-                c0, c1 = what[2:] if len(what) > 2 else (0, H)
-                q_cols((n, kp), wq[n][0][:, kp, c0:c1], wq[n][1][:, kp, c0:c1], c0, c1, E4M3X4)
-            elif kind == "qin":
-                g = what[1]
-                q_cols("in", iq[:, g, 0:I], isc[:, g, 0:I], g * I, (g + 1) * I, E4M3X4)
-            elif kind == "qh":
-                g, c0, c1 = what[1:]
-                q_cols("h%d" % g, iq[:, g, I + c0:I + c1], isc[:, g, I + c0:I + c1], c0, c1, E4M3X4)
-            elif kind == "qd":
-                g, n, c0, c1 = what[1:]
-                q_cols(("d", g, n), dq[:, g, n * NB + c0:n * NB + c1], dsc[:, g, n * NB + c0:n * NB + c1], c0, c1, E5M2X4)
-            elif kind == "x":
-                for b in range(what[1], what[2]):
-                    out1(b, eng)
-            elif kind == "out0":
-                pe_out0(what[1])
-            elif kind == "out":
-                v_out(what[1])
-            elif kind == "load":
-                (load_in if what[1] == "in" else lambda: load_w(*what[1]))()
-
-        def fills(eng, table, *key):
-            for w in table.get(key, []):
-                fill(eng, w)
+                V.tensor_copy(out=dst, in_=o_ps[b][:])
+            Q.dma_start(out=out_1[cols(m, P), cols(n)], in_=dst)
 
         load_az(0)
-        load_g(0)
         load_ah(0)
-        load_h(0)
-        load_w("h", 0)
+        load_g(0)
+        load_h(0, 0, 1)
         load_az(1)
-        load_g(1)
         load_ah(1)
-        load_h(1)
+        load_h(0, 1, PACK)
+        load_g(1)
+        load_w("h", 0)
+        V.memset(half[:], 0.5)
+        make_identity(nc, ident[:])
         s_p(0)
         s_qh(0)
         s_qz(0)
-        s_nh(0)
-        for k in range(TILES + 1):
-            a = k if k < TILES else None
-            m = k - 1 if k > 0 else None
-            n = k + 1 if k + 1 < TILES else None
-            if k + 2 < TILES:
-                load_az(k + 2)
-                load_g(k + 2)
-                load_ah(k + 2)
-                load_h(k + 2)
-            fills(Q, LOADS, k)
-            if a is not None:
-                v_u(a)
-                v_A(a)
-                gz(G, a, 0)
-            if n is not None:
-                s_p(n)
-                s_qh(n)
-            if m is not None:
-                v_B(m)
-                v_qA(m)
-            if a is not None:
-                gz(V, a, 1)
-                aT[a] = s_words(("a", a))
-            if n is not None:
-                s_qz(n)
-            fills(S, S1, k, 0)
-            if a is not None:
-                v_mz(a)
-                v_ht(a)
-                v_gm(a)
-            if m is not None:
-                v_qB(m)
-            if n is not None:
-                s_nh(n)
-            fills(S, S1, k, 1)
-            fills(V, V1, k, 0)
-            if a is not None:
-                gT[a] = s_words(("g", a))
-            fills(V, V1, k, 1)
+        load_az(2)
+        load_g(2)
+        load_w("h", 1)
+        load_g(3)
 
-        for j in range(9):
-            if j + 2 < 8 and j > 0:
-                load_ar(j + 2)
-            fills(Q, LOADS, "u", j)
-            if j == 0:
-                for x in range(3):
-                    load_ar(x)
-                s_r(0)
+        def front(k):
+            nxt = k + 1 < TILES
+            v_clip(k)
+            if k + 2 < TILES:
+                load_ah(k + 2)
+            if nxt:
+                s_p(k + 1)
+                s_qh(k + 1)
+            v_u(k)
+            if k == 0:
+                negate_h(V, 0)
+            pe_e(k)
+            v_mz(k)
+            if k > 0:
+                q_dz2(k - 1)
+            if k == 4:
                 pe_d(0)
-                v_mr(0)
-                v_hm(0)
-            if j < 8:
-                v_ED(j)
-            if j + 1 < 8:
-                pe_d(j + 1)
-                s_r(j + 1)
-            fills(S, S2, j, 0)
-            fills(V, V2, j, 0)
-            if j > 0:
-                v_qD(j - 1)
-            if j < 8:
-                s_cD(j)
-            if j + 1 < 8:
-                v_mr(j + 1)
-            fills(V, V2, j, 1)
-            if j + 1 < 8:
-                v_hm(j + 1)
-            fills(S, S2, j, 1)
-            fills(V, V2, j, 2)
-            fills(S, S2, j, 2)
+            v_dz2(k)
+            if nxt:
+                s_qz(k + 1)
+                if k + 3 < TILES:
+                    load_az(k + 3)
+                negate_h(S, k + 1)
+            if k > 1:
+                q_daz(k - 2)
+            v_gm(k)
+            dz2_t[k] = s_words(("a", k))
+            gm_t[k] = s_words(("g", k))
+
+        def daz(k):
+            v_daz(k, 0)
+            v_daz(k, 1)
+
+        front(0)
+        il(V, ("hp", 0, 0))
+        less_g(V, 0)
+        load_g(4)
+        il(S, ("hp", 0, 1))
+        il(V, ("h", 0, 0))
+        qe(("hp", 0, 0))
+
+        front(1)
+        less_g(G, 1, cols(0))
+        daz(0)
+        il(S, ("h", 0, 1))
+        less_g(V, 1, cols(1))
+        load_g(5)
+        qe(("h", 0, 0))
+        qe(("hp", 0, 1))
+        il(V, ("h", 1, 0))
+        load_ar(0)
+        load_h(1, 0, PACK)
+
+        front(2)
+        less_g(G, 2, cols(0))
+        daz(1)
+        qe(("h", 0, 1))
+        load_w("z", 0)
+        less_g(V, 2, cols(1))
+        load_g(6)
+        il(V, ("h", 1, 1))
+        load_w("z", 1)
+        qe(("h", 1, 0))
+        s_qr(0)
+
+        front(3)
+        s_r(0)
+        less_g(G, 3, cols(0))
+        daz(2)
+        qe(("h", 1, 1))
+        less_g(V, 3, cols(1))
+        load_g(7)
+        load_ar(1)
+        v_mr(0)
+        il(S, ("z", 0, 0))
+        v_hm(0)
+
+        front(4)
+        s_qr(1)
+        il(S, ("z", 0, 1))
+        load_w("r", 0)
+        s_r(1)
+        v_pair(0)
+        pe_d(1)
+        daz(3)
+        qe(("z", 0, 0))
+        il(V, ("z", 1, 0))
+        q_tok(0)
+        v_mr(1)
+        qe(("z", 0, 1))
+        v_hm(1)
+
+        front(5)
+        s_qr(2)
+        il(S, ("z", 1, 1))
+        load_w("r", 1)
+        s_r(2)
+        s_qr(3)
+        v_pair(1)
+        load_ar(2)
+        pe_d(2)
+        pe_turn(0)
+        daz(4)
+        qe(("z", 1, 0))
+        il(V, ("r", 0, 0))
+        q_tok(1)
+        v_mr(2)
+        qe(("z", 1, 1))
+        v_hm(2)
+        s_turn(0, 0)
+        s_r(3)
+        s_turn(0, 1)
+        v_pair(2)
+        pe_d(3)
+
+        front(6)
+        il(S, ("r", 0, 1))
+        load_inputs()
+        v_mr(3)
+        qe(("r", 0, 0))
+        v_hm(3)
+        il(S, ("r", 1, 0))
+        q_tok(2)
+        q_feat(0)
+        v_pair(3)
+        load_ar(3)
+        pe_turn(1)
+        daz(5)
+        qe(("r", 0, 1))
+        il(S, ("r", 1, 1))
+        q_tok(3)
+        qe(("r", 1, 0))
+        s_turn(1, 0)
+        s_turn(1, 1)
+        il(S, ("hp", 1, 0))
+
+        front(7)
+        s_qr(4)
+        il(S, ("hp", 1, 1))
+        s_r(4)
+        daz(6)
+        qe(("r", 1, 1))
+        q_feat(1)
+        for n in range(2):
+            pe_out0(0, n, n)
+        qe(("hp", 1, 0))
+        v_mr(4)
+        q_dz2(7)
+        pe_d(4)
+        v_hm(4)
+        s_qr(5)
+        il(S, ("in", 0))
+        s_r(5)
+        qe(("hp", 1, 1))
+        q_daz(6)
+        daz(7)
+        for n in range(2):
+            pe_out0(1, n, 2 + n)
+        for n in range(2):
+            v_out0(0, n)
+            pe_out0(2, n, n)
+
+        s_qr(6)
+        il(S, ("in", 1))
+        s_r(6)
+        v_pair(4)
+        pe_d(5)
+        for n in range(2):
+            v_out0(1, n)
+            pe_out0(3, n, 2 + n)
+        v_mr(5)
+        q_tok(4)
+        v_hm(5)
+        q_daz(7)
+        qe(("in", 0))
+        for n in range(2):
+            v_out0(2, n)
+            pe_out1(n)
+        s_qr(7)
+        v_pair(5)
+        pe_d(6)
+        for n in range(2):
+            v_out0(3, n)
+        pe_turn(2)
+        pe_out1(2)
+        pe_out1(3)
+        out1(S, 0)
+        s_r(7)
+        out1(S, 1)
+        v_mr(6)
+        q_tok(5)
+        v_hm(6)
+        qe(("in", 1))
+        s_turn(2, 0)
+        s_turn(2, 1)
+        pe_out1(4)
+        pe_out1(5)
+        out1(S, 2)
+        out1(S, 3)
+        plus_g(4, 0)
+        plus_g(5, 0)
+        pe_out1(6)
+        pe_out1(7)
+        v_pair(6)
+        pe_d(7)
+        out1(V, 4)
+        out1(V, 5)
+        pe_out1(8)
+        pe_out1(9)
+        out1(S, 6)
+        out1(S, 7)
+        v_mr(7)
+        q_tok(6)
+        v_hm(7)
+        q_feat(2)
+        for b in range(10, 18):
+            pe_out1(b)
+            out1(S, b - 2)
+        plus_g(6, 0)
+        plus_g(7, 0)
+        v_pair(7)
+        out1(V, 16)
+        out1(V, 17)
+        q_tok(7)
+
+        for n in range(2):
+            pe_out0(4, n, 2 + n, range(3))
+        pe_turn(3)
+        s_turn(3, 0)
+        s_turn(3, 1)
+        plus_g(4, 1)
+        plus_g(5, 1)
+        for n in range(2):
+            pe_out1(18 + n, 6 + n)
+        for n in range(2):
+            pe_out0(5, n, n, range(3))
+        plus_g(6, 1)
+        plus_g(7, 1)
+        q_feat(3, 0, 1)
+        for n in range(4):
+            pe_out0(4 + n // 2, n % 2, None, range(3, 4))
+        q_feat(3, 1, 2)
+        for n in range(2):
+            out1(S, 18 + n)
+            pe_out1(20 + n, 4 + n)
+        for n in range(2):
+            pe_out0(6, n, 6 + n)
+        for n in range(2):
+            out1(S, 20 + n)
+            pe_out1(22 + n, 4 + n)
+        for n in range(4):
+            v_out0(4 + n // 2, n % 2)
+        for n in range(2):
+            pe_out0(7, n, 2 + n)
+            out1(S, 22 + n)
+        for n in range(4):
+            v_out0(6 + n // 2, n % 2)

@@ -23,7 +23,6 @@ PACK = 4
 NB = 512
 KP = 2
 TILES = 8
-PAIR = 2 * P
 
 SIXTH = 1.0 / 6.0
 EDGE = 1.0 + 2.0 ** -8
@@ -62,17 +61,13 @@ def tile_grucell_v_kernel(
         ident = sb([P, P], F32, "ident")
 
         w_scales = {n: sb([P, KP, H], U8, "ws" + n) for n in "hzr"}
-        w_codes = {n: sb([P, KP, H], U32, "wc" + n) for n in "hz"}
+        w_codes = {n: sb([P, KP, H], U32, "wc" + n) for n in "hzr"}
         ih_codes, ih_scales = sb([P, KP, C], U32, "ihc"), sb([P, KP, C], U8, "ihs")
-        dz2_codes, dz2_scales = sb([P, TILES, KP * P], U32, "dz2c"), sb([P, TILES, KP * P], U8, "dz2s")
-        daz_codes, daz_scales = sb([P, TILES, KP * P], U32, "dazc"), sb([P, TILES, KP * P], U8, "dazs")
-        dar_scales = [sb([P, 2, H], U8, "dars%d" % g) for g in range(KP)]
-        dar_codes = {0: sb([P, 2, H], U32, "darc0")}
-        terms = [sb([P, PACK, H], F32, "terms%d" % g) for g in range(KP)]
+        tok_codes, tok_scales = sb([P, KP, H], U32, "tokc"), sb([P, KP, H], U8, "toks")
 
-        az, ah, gg, raw, h_nat, h_il, grouped = {}, {}, {}, {}, {}, {}, {}
+        az, ah, gg, raw, h_nat, terms, grouped = {}, {}, {}, {}, {}, {}, {}
         qh, qz, clip, neg_h, e_ps, dz2_t, gm_t, daz_t, words_ps = {}, {}, {}, {}, {}, {}, {}, {}, {}
-        ar, hm, d_ps, turn_ps, dar_t, o_ps = {}, {}, {}, {}, {}, {}
+        ar, dar, d_ps, dar_t, o_ps, dz2_q, daz_q, dar_q = {}, {}, {}, {}, {}, {}, {}, {}
 
         def load_az(i):
             az[i] = sb([P, H], F32, "az", 2)
@@ -83,12 +78,12 @@ def tile_grucell_v_kernel(
             Q.dma_start(out=ah[i][:], in_=ah_h[:, i // 4, i % 4, :])
 
         def load_g(i):
-            gg[i] = sb([P, H], BF16, "gg", 4)
+            gg[i] = sb([P, H], BF16, "gg", 3)
             Q.dma_start(out=gg[i][:], in_=g_h[:, i // 4, i % 4, :])
 
         def load_h(g, t0, t1):
             if t0 == 0:
-                h_nat[g] = sb([P, PACK, H], BF16, ("wcr", "darc1")[g])
+                h_nat[g] = sb([P, PACK, H], BF16, "hnat", 2)
             Q.dma_start(out=h_nat[g][:, t0:t1, :], in_=h_h[:, g, t0:t1, :])
 
         def load_w(n, kp):
@@ -99,9 +94,9 @@ def tile_grucell_v_kernel(
             raw["in"] = sb([P, KP, PACK, I], BF16, "raw", 2)
             Q.dma_start(out=raw["in"][:], in_=in_h)
 
-        def load_ar(x):
-            ar[x] = sb([P, PACK, NB], F32, "ar", 2)
-            Q.dma_start(out=ar[x][:], in_=ar_h[:, x // KP, :, cols(x % KP)])
+        def load_ar(i):
+            ar[i] = sb([P, H], F32, "ar", 3)
+            Q.dma_start(out=ar[i][:], in_=ar_h[:, i // 4, i % 4, :])
 
         def quant(codes, scales, src, fmt):
             V.quantize_mx(out=codes.bitcast(fmt), scales=scales, in_=src)
@@ -114,34 +109,37 @@ def tile_grucell_v_kernel(
             else:
                 V.tensor_copy(out=dst, in_=src)
 
-        def il(eng, key):
-            if key[0] == "hp":
-                g, n = key[1:]
-                if n == 0:
-                    h_il[g] = sb([P, H * PACK], BF16, "hil")
-                interleave(eng, h_il[g][:, cols(n, NB * PACK)], h_nat[g][:, :, cols(n)])
-                return
-            grouped[key] = sb([P, NB * PACK], BF16, "grouped", 2)
-            src = raw["in"][:, key[1]] if key[0] == "in" else raw[key[0], key[1]][:, :, cols(key[2])]
+        def il(eng, key, tag=("grouped", 3)):
+            name, g, n = key
+            grouped[key] = sb([P, NB * PACK], BF16, *tag)
+            if name == "in":
+                src = raw["in"][:, g]
+            else:
+                src = {"hp": h_nat, "dar": dar}[name][g] if name in ("hp", "dar") else raw[name, g]
+                src = src[:, :, cols(n)]
             interleave(eng, grouped[key][:], src)
 
         def qe(key):
-            if key[0] == "hp":
-                g, n = key[1:]
-                at = slice(I + n * NB, I + (n + 1) * NB)
-                quant(ih_codes[:, g, at], ih_scales[:, g, at], h_il[g][:, cols(n, NB * PACK)], E4M3X4)
-            elif key[0] == "in":
-                quant(ih_codes[:, key[1], 0:I], ih_scales[:, key[1], 0:I], grouped[key][:], E4M3X4)
+            name, g, n = key
+            if name == "dar":
+                quant(tok_codes[:, g, cols(n)], tok_scales[:, g, cols(n)], grouped[key][:], E5M2X4)
+            elif name in ("in", "hp"):
+                at = cols(0 if name == "in" else 1 + n)
+                quant(ih_codes[:, g, at], ih_scales[:, g, at], grouped[key][:], E4M3X4)
             else:
-                n, kp, x = key
-                if n not in w_codes:
-                    w_codes[n] = sb([P, KP, H], U32, "wc" + n)
-                quant(w_codes[n][:, kp, cols(x)], w_scales[n][:, kp, cols(x)], grouped[key][:], E4M3X4)
+                quant(w_codes[name][:, g, cols(n)], w_scales[name][:, g, cols(n)], grouped[key][:], E4M3X4)
+
+        def quant_turned(tag, bufs, src):
+            codes, scales = sb([P, 2, P], U32, tag + "c", bufs), sb([P, 2, P], U8, tag + "s", bufs)
+            quant(codes[:].rearrange("p k r -> p (k r)"), scales[:].rearrange("p k r -> p (k r)"),
+                  src[:].rearrange("p k r s -> p (k r s)"), E5M2X4)
+            return [(codes[:, k], scales[:, k]) for k in range(2)]
 
         def term(i):
-            return terms[i // 4][:, i % 4, :]
+            return terms[i][:]
 
         def s_p(i):
+            terms[i] = sb([P, H], F32, "terms", 7)
             S.activation(out=term(i), in_=az[i][:], func=ACT.Relu, bias=half[:], scale=-SIXTH)
 
         def s_qh(i):
@@ -162,51 +160,53 @@ def tile_grucell_v_kernel(
                 V.tensor_scalar(out=dst, in0=src, scalar1=-1.0, scalar2=None, op0=ALU.mult)
 
         def v_clip(i):
-            clip[i] = sb([P, PACK, KP * P], F32, "clip")
+            clip[i] = sb([P, PACK, KP * P], F32, "clip", 2)
             V.tensor_scalar(out=clip[i][:].rearrange("p s n -> p n s"), in0=ah[i][:].rearrange("p (n s) -> p n s", s=PACK),
                             scalar1=-1.0, scalar2=1.0, op0=ALU.max, op1=ALU.min)
 
         def pe_e(i):
             for kp in range(KP):
-                e_ps[i, kp] = bank(2 * (i % 2) + kp)
+                e_ps[i, kp] = bank(kp)
                 for s in range(PACK):
                     for src, first in ((clip, True), (neg_h, False)):
                         PE.matmul(out=e_ps[i, kp][:, cols(s, P)], lhsT=src[i][:, s, cols(kp, P)], rhs=ident[:],
                                   start=first, stop=not first, is_transpose=True)
 
-        def turn_words(key, src, n):
+        def turn_words(key, halves, n):
             words_ps[key] = bank(n)
-            w = src.bitcast(F32)
-            for kp in range(KP):
+            for k, src in enumerate(halves):
+                w = src.bitcast(F32)
                 for u in range(2):
-                    PE.transpose(words_ps[key][:, cols(2 * kp + u, P)], w[:, 256 * kp + u:256 * (kp + 1):2], ident[:])
+                    PE.transpose(words_ps[key][:, cols(2 * k + u, P)], w[:, u::2], ident[:])
 
-        def s_words(key):
+        def copy(eng, dst, src):
+            if eng is S:
+                S.copy(out=dst, in_=src)
+            else:
+                V.tensor_copy(out=dst, in_=src)
+
+        def take_words(eng, key):
             out = sb([P, KP, P, PACK], BF16, "turned" + key[0], 2)
-            S.copy(out=out[:].bitcast(F32), in_=words_ps[key][:].rearrange("p (k u r) -> p k r u", k=KP, u=2))
-            return out
+            copy(eng, out[:].bitcast(F32), words_ps[key][:].rearrange("p (k u r) -> p k r u", k=KP, u=2))
+            {"a": dz2_t, "g": gm_t, "d": dar_t}[key[0]][key[1]] = out
 
         def v_u(i):
             V.scalar_tensor_tensor(out=term(i), in0=term(i), scalar=1.0, in1=gg[i][:], op0=ALU.min, op1=ALU.mult)
 
         def v_dz2(i):
             V.scalar_tensor_tensor(out=qh[i][:], in0=qh[i][:], scalar=EDGE, in1=term(i), op0=ALU.is_lt, op1=ALU.mult)
-            turn_words(("a", i), qh[i][:], 4)
+            turn_words(("a", i), [qh[i][:, cols(n)] for n in range(2)], 2)
 
         def v_mz(i):
             V.tensor_scalar(out=qz[i][:], in0=qz[i][:], scalar1=EDGE, scalar2=None, op0=ALU.is_lt)
 
         def v_gm(i):
             V.tensor_tensor(out=qz[i][:], in0=qz[i][:], in1=gg[i][:], op=ALU.mult)
-            turn_words(("g", i), qz[i][:], 5)
+            turn_words(("g", i), [qz[i][:, cols(n)] for n in range(2)], 3)
 
         def less_g(eng, i, at=slice(0, H)):
             y = term(i)[:, at]
             eng.tensor_tensor(out=y, in0=y, in1=gg[i][:, at], op=ALU.subtract)
-
-        def plus_g(i, n):
-            y = term(i)[:, cols(n)]
-            V.tensor_tensor(out=y, in0=y, in1=gg[i][:, cols(n)], op=ALU.add)
 
         def v_daz(i, kp):
             if kp == 0:
@@ -215,118 +215,87 @@ def tile_grucell_v_kernel(
                                    scalar=-SIXTH, in1=gm_t[i][:, kp], op0=ALU.mult, op1=ALU.mult)
 
         def q_dz2(i):
-            quant(dz2_codes[:, i], dz2_scales[:, i], dz2_t[i][:].rearrange("p k r s -> p (k r s)"), E5M2X4)
+            dz2_q[i] = quant_turned("dz2", 3, dz2_t[i])
 
         def q_daz(i):
-            quant(daz_codes[:, i], daz_scales[:, i], daz_t[i][:].rearrange("p k r s -> p (k r s)"), E5M2X4)
+            daz_q[i] = quant_turned("dazq", 4, daz_t[i])
 
-        def s_qr(j):
-            x, at = j // 2, cols(j % 2, PAIR)
-            if j % 2 == 0:
-                hm[x] = sb([P, NB * PACK], BF16, "hm", 2)
-            S.activation(out=hm[x][:, cols(j % 2, PAIR * PACK)].rearrange("p (c i t) -> p c t i", i=4, t=PACK),
-                         in_=ar[x][:, :, at].rearrange("p t (c i) -> p c t i", i=4), func=ACT.Square, scale=ROOT_3)
+        def s_qr(i, at=slice(0, H)):
+            if i % 4 == 0:
+                dar[i // 4] = sb([P, PACK, H], BF16, "dar", 2)
+            S.activation(out=dar[i // 4][:, i % 4, at], in_=ar[i][:, at], func=ACT.Square, scale=ROOT_3)
 
-        def s_r(j):
-            x, at = j // 2, cols(j % 2, PAIR)
-            S.activation(out=ar[x][:, :, at], in_=ar[x][:, :, at], func=ACT.Relu, bias=half[:], scale=SIXTH)
+        def s_r(i, at=slice(0, H)):
+            S.activation(out=ar[i][:, at], in_=ar[i][:, at], func=ACT.Relu, bias=half[:], scale=SIXTH)
 
-        def v_mr(j):
-            y = hm[j // 2][:, cols(j % 2, PAIR * PACK)]
+        def v_mr(i, tiles=1, at=slice(0, H)):
+            y = dar[i // 4][:, i % 4:i % 4 + tiles, at]
             V.tensor_scalar(out=y, in0=y, scalar1=EDGE, scalar2=None, op0=ALU.is_lt)
 
-        def v_hm(j):
-            y = hm[j // 2][:, cols(j % 2, PAIR * PACK)]
-            V.tensor_tensor(out=y, in0=y, in1=h_il[j // 4][:, cols(j % 4, PAIR * PACK)], op=ALU.mult)
+        def v_hm(i, tiles=1, at=slice(0, H)):
+            y = dar[i // 4][:, i % 4:i % 4 + tiles, at]
+            V.tensor_tensor(out=y, in0=y, in1=h_nat[i // 4][:, i % 4:i % 4 + tiles, at], op=ALU.mult)
 
-        def pe_d(j):
-            for b in range(2):
-                d_ps[j, b] = bank(6 + b)
-                at = cols(2 * (j % 4) + b, P)
-                for t in range(PACK):
-                    i = PACK * (j // 4) + t
-                    for kp in range(KP):
-                        PE.matmul_mx(
-                            out=d_ps[j, b][:, cols(t, P)],
-                            lhsT=dz2_codes[:, i, cols(kp, P)].bitcast(E5M2X4), lhsT_scale=dz2_scales[:, i, cols(kp, P)],
-                            rhs=w_codes["h"][:, kp, at].bitcast(E4M3X4), rhs_scale=w_scales["h"][:, kp, at],
-                            start=kp == 0, stop=kp == KP - 1,
-                        )
+        def pe_d(units, first_bank=4):
+            for b, (i, n) in enumerate(units):
+                d_ps[i, n] = bank(first_bank + b)
+                for kp in range(KP):
+                    codes, scales = dz2_q[i][kp]
+                    PE.matmul_mx(
+                        out=d_ps[i, n][:], lhsT=codes.bitcast(E5M2X4), lhsT_scale=scales,
+                        rhs=w_codes["h"][:, kp, cols(n)].bitcast(E4M3X4), rhs_scale=w_scales["h"][:, kp, cols(n)],
+                        start=kp == 0, stop=kp == KP - 1,
+                    )
 
-        def v_pair(j):
-            x = j // 2
-            for b in range(2):
-                r = ar[x][:, :, cols(2 * (j % 2) + b, P)]
-                V.scalar_tensor_tensor(out=r, in0=r, scalar=1.0, in1=d_ps[j, b][:].rearrange("p (t c) -> p t c", t=PACK),
-                                       op0=ALU.min, op1=ALU.mult)
-                y = terms[j // 4][:, :, cols(2 * (j % 4) + b, P)]
-                G.tensor_tensor(out=y, in0=r, in1=y, op=ALU.subtract)
-            for b in range(2):
-                y = hm[x][:, cols(2 * (j % 2) + b, NB)].rearrange("p (c t) -> p c t", t=PACK)
-                V.scalar_tensor_tensor(out=y, in0=d_ps[j, b][:].rearrange("p (t c) -> p c t", t=PACK), scalar=SIXTH, in1=y,
-                                       op0=ALU.mult, op1=ALU.mult)
+        def v_dr(units):
+            for i, n in units:
+                r = ar[i][:, cols(n)]
+                V.scalar_tensor_tensor(out=r, in0=r, scalar=1.0, in1=d_ps[i, n][:], op0=ALU.min, op1=ALU.mult)
 
-        def q_tok(j):
-            g, at = j // 4, cols(j % 4, PAIR)
-            if g not in dar_codes:
-                dar_codes[g] = sb([P, 2, H], U32, "darc%d" % g)
-            quant(dar_codes[g][:, 0, at], dar_scales[g][:, 0, at], hm[j // 2][:, cols(j % 2, PAIR * PACK)], E5M2X4)
+        def add_dr(eng, i, at=slice(0, H)):
+            y = terms[i][:, at]
+            eng.tensor_tensor(out=y, in0=ar[i][:, at], in1=y, op=ALU.subtract)
 
-        def pe_turn(x):
-            w = hm[x][:].bitcast(F32)
-            for tp in range(2):
-                turn_ps[x, tp] = bank(4 + tp)
-                for s in range(PACK):
-                    PE.transpose(turn_ps[x, tp][:, cols(s, P)], w[:, 2 * s + tp::8], ident[:])
+        def v_dar(units, at_bank=2):
+            for i, n in units:
+                y = dar[i // 4][:, i % 4, cols(n)]
+                V.scalar_tensor_tensor(out=y, in0=d_ps[i, n][:], scalar=SIXTH, in1=y, op0=ALU.mult, op1=ALU.mult)
+            turn_words(("d", units), [dar[i // 4][:, i % 4, cols(n)] for i, n in units], at_bank)
 
-        def s_turn(x, tp):
-            if tp == 0:
-                dar_t[x] = sb([P, 2, 2 * P * PACK], BF16, "dart")
-            S.copy(out=dar_t[x][:, tp].rearrange("p (e r s) -> p e r s", e=2, s=PACK),
-                   in_=turn_ps[x, tp][:].bitcast(BF16).rearrange("p (s r e) -> p e r s", s=PACK, e=2))
+        def q_dar(units):
+            for unit, operand in zip(units, quant_turned("darq", 4, dar_t[units])):
+                dar_q[unit] = operand
 
-        def q_feat(x, tp0=0, tp1=2):
-            g, at = x // KP, slice((x % KP) * NB + tp0 * PAIR, (x % KP) * NB + tp1 * PAIR)
-            quant(dar_codes[g][:, 1, at], dar_scales[g][:, 1, at], dar_t[x][:, tp0:tp1].rearrange("p a b -> p (a b)"), E5M2X4)
+        def pe_out0(i, first_bank=6):
+            for n in range(2):
+                o_ps[i, n] = bank(first_bank + n)
+                for k in range(2 * KP):
+                    kp = k % KP
+                    codes, scales = daz_q[i][kp] if k < KP else dar_q[i, kp]
+                    gate = "z" if k < KP else "r"
+                    PE.matmul_mx(
+                        out=o_ps[i, n][:], lhsT=codes.bitcast(E5M2X4), lhsT_scale=scales,
+                        rhs=w_codes[gate][:, kp, cols(n)].bitcast(E4M3X4), rhs_scale=w_scales[gate][:, kp, cols(n)],
+                        start=k == 0, stop=k == 2 * KP - 1,
+                    )
 
-        def pe_out0(i, n, at_bank, passes=range(2 * KP)):
-            g, t = i // 4, i % 4
-            if passes[0] == 0:
-                o_ps[i, n] = bank(at_bank)
-            for k in passes:
-                kp = k % KP
-                if k < KP:
-                    codes, scales = daz_codes[:, i, cols(kp, P)], daz_scales[:, i, cols(kp, P)]
-                else:
-                    at = cols(PACK * kp + t, P)
-                    codes, scales = dar_codes[g][:, 1, at], dar_scales[g][:, 1, at]
-                gate = "z" if k < KP else "r"
-                PE.matmul_mx(
-                    out=o_ps[i, n][:], lhsT=codes.bitcast(E5M2X4), lhsT_scale=scales,
-                    rhs=w_codes[gate][:, kp, cols(n)].bitcast(E4M3X4), rhs_scale=w_scales[gate][:, kp, cols(n)],
-                    start=k == 0, stop=k == 2 * KP - 1,
-                )
-
-        def v_out0(i, n):
-            y = terms[i // 4][:, i % 4, cols(n)]
-            V.tensor_tensor(out=y, in0=o_ps[i, n][:], in1=y, op=ALU.add)
-            Q.dma_start(out=o0_h[:, i // 4, i % 4, cols(n)], in_=y)
+        def v_out0(i):
+            for n in range(2):
+                y = terms[i][:, cols(n)]
+                V.tensor_tensor(out=y, in0=o_ps[i, n][:], in1=y, op=ALU.add)
+                Q.dma_start(out=o0_h[:, i // 4, i % 4, cols(n)], in_=y)
 
         stage = {}
 
-        blocks = []
-        for j in range(4):
-            blocks.extend([(m, n) for m in (2 * j, 2 * j + 1) for n in range(1 if j < 2 else 0, 3)])
-            if j in (1, 2):
-                blocks.extend([(m, 0) for m in (2 * j - 2, 2 * j - 1)])
+        blocks = [(m, n) for x in range(2) for n in (1, 2, 0) for m in range(4 * x, 4 * x + 4)]
 
-        def pe_out1(b, at_bank=None):
+        def pe_out1(b, at_bank):
             m, n = blocks[b]
-            o_ps[b] = bank(b % 4 if at_bank is None else at_bank)
+            o_ps[b] = bank(at_bank)
             for g in range(KP):
                 PE.matmul_mx(
                     out=o_ps[b][:],
-                    lhsT=dar_codes[g][:, 0, cols(m, P)].bitcast(E5M2X4), lhsT_scale=dar_scales[g][:, 0, cols(m, P)],
+                    lhsT=tok_codes[:, g, cols(m, P)].bitcast(E5M2X4), lhsT_scale=tok_scales[:, g, cols(m, P)],
                     rhs=ih_codes[:, g, cols(n)].bitcast(E4M3X4), rhs_scale=ih_scales[:, g, cols(n)],
                     start=g == 0, stop=g == KP - 1,
                 )
@@ -334,13 +303,36 @@ def tile_grucell_v_kernel(
         def out1(eng, b):
             m, n = blocks[b]
             if b % 2 == 0:
-                stage[b // 2] = sb([P, 2, NB], F32, ("az", "ah")[b // 2 % 2], 2)
+                stage[b // 2] = sb([P, 2, NB], F32, *(("az", 2), ("ah", 2), ("clip", 2))[b // 2 % 3])
             dst = stage[b // 2][:, b % 2, :]
-            if eng is S:
-                S.copy(out=dst, in_=o_ps[b][:])
-            else:
-                V.tensor_copy(out=dst, in_=o_ps[b][:])
+            copy(eng, dst, o_ps[b][:])
             Q.dma_start(out=out_1[cols(m, P), cols(n)], in_=dst)
+
+        def both(i):
+            return ((i, 0), (i, 1))
+
+        def front(k):
+            v_clip(k)
+            if k + 2 < TILES:
+                load_ah(k + 2)
+            v_u(k)
+            if k == 0:
+                negate_h(V, 0)
+            v_mz(k)
+            if k > 0:
+                q_dz2(k - 1)
+            v_dz2(k)
+            if k > 1:
+                q_daz(k - 2)
+            v_gm(k)
+
+        def turned(k):
+            take_words(S, ("a", k))
+            take_words(S, ("g", k))
+
+        def daz(k):
+            v_daz(k, 0)
+            v_daz(k, 1)
 
         load_az(0)
         load_ah(0)
@@ -348,273 +340,214 @@ def tile_grucell_v_kernel(
         load_h(0, 0, 1)
         load_az(1)
         load_ah(1)
-        load_h(0, 1, PACK)
-        load_g(1)
         load_w("h", 0)
+        load_h(0, 1, 2)
+        load_g(1)
+        load_w("h", 1)
         V.memset(half[:], 0.5)
         make_identity(nc, ident[:])
         s_p(0)
         s_qh(0)
         s_qz(0)
         load_az(2)
-        load_g(2)
-        load_w("h", 1)
-        load_g(3)
-
-        def front(k):
-            nxt = k + 1 < TILES
-            v_clip(k)
-            if k + 2 < TILES:
-                load_ah(k + 2)
-            if nxt:
-                s_p(k + 1)
-                s_qh(k + 1)
-            v_u(k)
-            if k == 0:
-                negate_h(V, 0)
-            pe_e(k)
-            v_mz(k)
-            if k > 0:
-                q_dz2(k - 1)
-            if k == 4:
-                pe_d(0)
-            v_dz2(k)
-            if nxt:
-                s_qz(k + 1)
-                if k + 3 < TILES:
-                    load_az(k + 3)
-                negate_h(S, k + 1)
-            if k > 1:
-                q_daz(k - 2)
-            v_gm(k)
-            dz2_t[k] = s_words(("a", k))
-            gm_t[k] = s_words(("g", k))
-
-        def daz(k):
-            v_daz(k, 0)
-            v_daz(k, 1)
 
         front(0)
-        il(V, ("hp", 0, 0))
-        less_g(V, 0)
-        load_g(4)
-        il(S, ("hp", 0, 1))
-        il(V, ("h", 0, 0))
-        qe(("hp", 0, 0))
-
-        front(1)
-        less_g(G, 1, cols(0))
-        daz(0)
-        il(S, ("h", 0, 1))
-        less_g(V, 1, cols(1))
-        load_g(5)
-        qe(("h", 0, 0))
-        qe(("hp", 0, 1))
-        il(V, ("h", 1, 0))
+        pe_e(0)
         load_ar(0)
-        load_h(1, 0, PACK)
-
-        front(2)
-        less_g(G, 2, cols(0))
-        daz(1)
-        qe(("h", 0, 1))
+        load_h(0, 2, PACK)
+        load_g(2)
+        s_p(1)
+        s_qh(1)
+        s_qz(1)
+        load_az(3)
+        negate_h(S, 1)
+        turned(0)
+        less_g(V, 0)
+        load_g(3)
+        il(V, ("h", 0, 0))
+        il(V, ("h", 0, 1))
         load_w("z", 0)
-        less_g(V, 2, cols(1))
-        load_g(6)
+        qe(("h", 0, 0))
+        il(S, ("h", 1, 0))
+        qe(("h", 0, 1))
         il(V, ("h", 1, 1))
         load_w("z", 1)
-        qe(("h", 1, 0))
-        s_qr(0)
-
-        front(3)
-        s_r(0)
-        less_g(G, 3, cols(0))
-        daz(2)
-        qe(("h", 1, 1))
-        less_g(V, 3, cols(1))
-        load_g(7)
         load_ar(1)
+
+        front(1)
+        s_p(2)
+        s_qh(2)
+        s_qz(2)
+        load_az(4)
+        s_qr(0)
+        turned(1)
+        negate_h(S, 2)
+        less_g(G, 1, cols(0))
+        daz(0)
+        pe_e(1)
+        qe(("h", 1, 0))
+        less_g(V, 1, cols(1))
+        load_g(4)
+        qe(("h", 1, 1))
+        pe_d(both(0))
+        s_r(0)
         v_mr(0)
-        il(S, ("z", 0, 0))
+        il(V, ("z", 0, 0))
         v_hm(0)
-
-        front(4)
-        s_qr(1)
-        il(S, ("z", 0, 1))
-        load_w("r", 0)
-        s_r(1)
-        v_pair(0)
-        pe_d(1)
-        daz(3)
-        qe(("z", 0, 0))
-        il(V, ("z", 1, 0))
-        q_tok(0)
-        v_mr(1)
-        qe(("z", 0, 1))
-        v_hm(1)
-
-        front(5)
-        s_qr(2)
-        il(S, ("z", 1, 1))
-        load_w("r", 1)
-        s_r(2)
-        s_qr(3)
-        v_pair(1)
         load_ar(2)
-        pe_d(2)
-        pe_turn(0)
-        daz(4)
-        qe(("z", 1, 0))
-        il(V, ("r", 0, 0))
-        q_tok(1)
-        v_mr(2)
-        qe(("z", 1, 1))
-        v_hm(2)
-        s_turn(0, 0)
-        s_r(3)
-        s_turn(0, 1)
-        v_pair(2)
-        pe_d(3)
+        load_h(1, 0, PACK)
 
-        front(6)
-        il(S, ("r", 0, 1))
-        load_inputs()
-        v_mr(3)
-        qe(("r", 0, 0))
-        v_hm(3)
-        il(S, ("r", 1, 0))
-        q_tok(2)
-        q_feat(0)
-        v_pair(3)
-        load_ar(3)
-        pe_turn(1)
-        daz(5)
-        qe(("r", 0, 1))
-        il(S, ("r", 1, 1))
-        q_tok(3)
-        qe(("r", 1, 0))
-        s_turn(1, 0)
-        s_turn(1, 1)
-        il(S, ("hp", 1, 0))
-
-        front(7)
-        s_qr(4)
-        il(S, ("hp", 1, 1))
-        s_r(4)
-        daz(6)
-        qe(("r", 1, 1))
-        q_feat(1)
-        for n in range(2):
-            pe_out0(0, n, n)
-        qe(("hp", 1, 0))
-        v_mr(4)
-        q_dz2(7)
-        pe_d(4)
-        v_hm(4)
-        s_qr(5)
-        il(S, ("in", 0))
-        s_r(5)
-        qe(("hp", 1, 1))
-        q_daz(6)
-        daz(7)
-        for n in range(2):
-            pe_out0(1, n, 2 + n)
-        for n in range(2):
-            v_out0(0, n)
-            pe_out0(2, n, n)
+        extra = {
+            2: ((S, ("z", 0, 1)), (V, ("z", 1, 0)), (S, ("z", 1, 1))),
+            3: ((S, ("r", 0, 1)), (V, ("r", 0, 0)), (S, ("r", 1, 0))),
+            4: (),
+            5: ((S, ("hp", 0, 0)),),
+            6: ((S, ("hp", 1, 0)),),
+        }
+        first, second = ((6, 0), (7, 0)), ((6, 1), (7, 1))
+        waiting = [("z", 0, 0)]
+        for k in range(2, TILES - 1):
+            b = k - 2
+            if k == 4:
+                qe(waiting.pop(0))
+                il(S, ("r", 1, 1))
+            s_qr(b + 1)
+            s_p(k + 1)
+            s_qh(k + 1)
+            s_qz(k + 1)
+            if k + 3 < TILES:
+                load_az(k + 3)
+            front(k)
+            if k == 4:
+                qe(waiting.pop(0))
+                qe(("r", 1, 0))
+                qe(("r", 1, 1))
+                pe_out0(0)
+            take_words(S, ("a", k))
+            s_r(b + 1)
+            take_words(S, ("g", k))
+            negate_h(S, k + 1)
+            less_g(G, k, cols(0) if k < 4 else slice(0, H))
+            v_dr(both(b))
+            add_dr(G, b)
+            v_dar(both(b))
+            load_ar(b + 3)
+            daz(k - 1)
+            if k >= 4:
+                v_out0(k - 4)
+            pe_d(both(b + 1))
+            pe_e(k)
+            take_words(S, ("d", both(b)))
+            if k < 4:
+                less_g(V, k, cols(1))
+            if k + 3 < TILES:
+                load_g(k + 3)
+            v_mr(b + 1)
+            for key in waiting:
+                qe(key)
+            waiting = []
+            if b > 0:
+                q_dar(both(b - 1))
+            v_hm(b + 1)
+            for eng, key in extra[k]:
+                il(eng, key)
+                if key != ("r", 1, 0):
+                    waiting.append(key)
+                if key[2] == 1 and key[0] == "z":
+                    load_w("r", key[1])
+                if key == ("r", 0, 0):
+                    load_inputs()
+                if len(waiting) == 3:
+                    qe(waiting.pop(0))
+            if k >= 4:
+                pe_out0(k - 3)
 
         s_qr(6)
-        il(S, ("in", 1))
-        s_r(6)
-        v_pair(4)
-        pe_d(5)
-        for n in range(2):
-            v_out0(1, n)
-            pe_out0(3, n, 2 + n)
-        v_mr(5)
-        q_tok(4)
-        v_hm(5)
-        q_daz(7)
-        qe(("in", 0))
-        for n in range(2):
-            v_out0(2, n)
-            pe_out1(n)
+        il(S, ("dar", 0, 0))
+        front(7)
+        take_words(S, ("a", 7))
         s_qr(7)
-        v_pair(5)
-        pe_d(6)
-        for n in range(2):
-            v_out0(3, n)
-        pe_turn(2)
-        pe_out1(2)
-        pe_out1(3)
-        out1(S, 0)
+        take_words(S, ("g", 7))
+        s_r(6)
+        less_g(G, 7)
+        v_dr(both(5))
+        add_dr(G, 5)
+        v_dar(both(5))
+        daz(6)
+        v_out0(3)
+        q_dz2(7)
+        pe_d(first)
+        pe_e(7)
+        take_words(S, ("d", both(5)))
+        qe(("hp", 1, 0))
+        il(S, ("hp", 0, 1))
+        v_mr(6, 2, cols(0))
+        qe(("dar", 0, 0))
+        il(S, ("hp", 1, 1))
+        q_dar(both(4))
+        v_hm(6, 2, cols(0))
+        pe_out0(4)
+        q_daz(6)
+
         s_r(7)
+        v_dar(first)
+        v_daz(7, 0)
+        il(V, ("dar", 1, 0))
+        take_words(S, ("d", first))
+        il(S, ("in", 0, 0), ("raw", 2))
+        v_daz(7, 1)
+        pe_d(second, 0)
+        qe(("dar", 1, 0))
+        pe_out1(0, 3)
+        pe_out1(1, 2)
+        q_dar(both(5))
+        v_dr(first)
+        pe_out1(2, 4)
+        pe_out1(3, 5)
+        v_out0(4)
+        pe_out0(5)
+        out1(S, 0)
         out1(S, 1)
-        v_mr(6)
-        q_tok(5)
-        v_hm(6)
-        qe(("in", 1))
-        s_turn(2, 0)
-        s_turn(2, 1)
-        pe_out1(4)
-        pe_out1(5)
+        qe(("hp", 0, 1))
         out1(S, 2)
         out1(S, 3)
-        plus_g(4, 0)
-        plus_g(5, 0)
-        pe_out1(6)
-        pe_out1(7)
-        v_pair(6)
-        pe_d(7)
-        out1(V, 4)
-        out1(V, 5)
-        pe_out1(8)
-        pe_out1(9)
-        out1(S, 6)
-        out1(S, 7)
-        v_mr(7)
-        q_tok(6)
-        v_hm(7)
-        q_feat(2)
-        for b in range(10, 18):
-            pe_out1(b)
-            out1(S, b - 2)
-        plus_g(6, 0)
-        plus_g(7, 0)
-        v_pair(7)
-        out1(V, 16)
-        out1(V, 17)
-        q_tok(7)
-
-        for n in range(2):
-            pe_out0(4, n, 2 + n, range(3))
-        pe_turn(3)
-        s_turn(3, 0)
-        s_turn(3, 1)
-        plus_g(4, 1)
-        plus_g(5, 1)
-        for n in range(2):
-            pe_out1(18 + n, 6 + n)
-        for n in range(2):
-            pe_out0(5, n, n, range(3))
-        plus_g(6, 1)
-        plus_g(7, 1)
-        q_feat(3, 0, 1)
-        for n in range(4):
-            pe_out0(4 + n // 2, n % 2, None, range(3, 4))
-        q_feat(3, 1, 2)
-        for n in range(2):
-            out1(S, 18 + n)
-            pe_out1(20 + n, 4 + n)
-        for n in range(2):
-            pe_out0(6, n, 6 + n)
-        for n in range(2):
-            out1(S, 20 + n)
-            pe_out1(22 + n, 4 + n)
-        for n in range(4):
-            v_out0(4 + n // 2, n % 2)
-        for n in range(2):
-            pe_out0(7, n, 2 + n)
-            out1(S, 22 + n)
-        for n in range(4):
-            v_out0(6 + n // 2, n % 2)
+        il(S, ("in", 1, 0))
+        v_mr(6, 2, cols(1))
+        qe(("hp", 1, 1))
+        v_hm(6, 2, cols(1))
+        ring = (3, 4, 5, 2)
+        for b in range(4, 7):
+            pe_out1(b, ring[b % 4])
+        q_dar(first)
+        v_dar(second)
+        take_words(S, ("d", second))
+        pe_out1(7, ring[3])
+        qe(("in", 0, 0))
+        qe(("in", 1, 0))
+        for b in range(4, 8):
+            out1(S, b)
+            pe_out1(b + 4, ring[b % 4])
+        il(S, ("dar", 0, 1))
+        il(V, ("dar", 1, 1))
+        q_dar(second)
+        v_out0(5)
+        pe_out0(6)
+        qe(("dar", 1, 1))
+        v_dr(second)
+        qe(("dar", 0, 1))
+        q_daz(7)
+        add_dr(V, 6)
+        ring = (0, 1, 3, 4, 5, 2)
+        for b in range(12, 18):
+            if b >= 14:
+                out1(S, b - 6)
+            pe_out1(b, ring[b % 6])
+        v_out0(6)
+        add_dr(V, 7)
+        pe_out0(7)
+        for b in range(12, 18):
+            out1(S, b)
+            pe_out1(b + 6, ring[b % 6])
+        v_out0(7)
+        for b in range(18, 24):
+            out1(V if b % 2 else S, b)

@@ -342,7 +342,6 @@ def tile_grucell_v_kernel(
         load_ah(1)
         load_w("h", 0)
         load_h(0, 1, 2)
-        load_g(1)
         load_w("h", 1)
         V.memset(half[:], 0.5)
         make_identity(nc, ident[:])
@@ -350,49 +349,49 @@ def tile_grucell_v_kernel(
         s_qh(0)
         s_qz(0)
         load_az(2)
+        load_g(1)
 
         front(0)
         pe_e(0)
         load_ar(0)
         load_h(0, 2, PACK)
-        load_g(2)
         s_p(1)
         s_qh(1)
         s_qz(1)
-        load_az(3)
         negate_h(S, 1)
         turned(0)
         less_g(V, 0)
-        load_g(3)
         il(V, ("h", 0, 0))
         il(V, ("h", 0, 1))
         load_w("z", 0)
+        load_ar(1)
+        load_az(3)
+        load_g(2)
         qe(("h", 0, 0))
         il(S, ("h", 1, 0))
         qe(("h", 0, 1))
         il(V, ("h", 1, 1))
-        load_w("z", 1)
-        load_ar(1)
 
         front(1)
+        load_w("z", 1)
+        load_g(3)
         s_p(2)
         s_qh(2)
         s_qz(2)
         load_az(4)
         s_qr(0)
+        il(S, ("z", 0, 0))
         turned(1)
         negate_h(S, 2)
-        less_g(G, 1, cols(0))
         daz(0)
         pe_e(1)
         qe(("h", 1, 0))
-        less_g(V, 1, cols(1))
+        less_g(V, 1)
         load_g(4)
+        v_mr(0)
         qe(("h", 1, 1))
         pe_d(both(0))
         s_r(0)
-        v_mr(0)
-        il(V, ("z", 0, 0))
         v_hm(0)
         load_ar(2)
         load_h(1, 0, PACK)
@@ -427,7 +426,8 @@ def tile_grucell_v_kernel(
             s_r(b + 1)
             take_words(S, ("g", k))
             negate_h(S, k + 1)
-            less_g(G, k, cols(0) if k < 4 else slice(0, H))
+            if k >= 4:
+                less_g(G, k, cols(0))
             v_dr(both(b))
             add_dr(G, b)
             v_dar(both(b))
@@ -438,8 +438,7 @@ def tile_grucell_v_kernel(
             pe_d(both(b + 1))
             pe_e(k)
             take_words(S, ("d", both(b)))
-            if k < 4:
-                less_g(V, k, cols(1))
+            less_g(V, k, cols(1) if k >= 4 else slice(0, H))
             if k + 3 < TILES:
                 load_g(k + 3)
             v_mr(b + 1)
@@ -457,19 +456,18 @@ def tile_grucell_v_kernel(
                     load_w("r", key[1])
                 if key == ("r", 0, 0):
                     load_inputs()
-                if len(waiting) == 3:
-                    qe(waiting.pop(0))
             if k >= 4:
                 pe_out0(k - 3)
 
         s_qr(6)
         il(S, ("dar", 0, 0))
+        il(S, ("dar", 0, 1), ("raw", 2))
         front(7)
         take_words(S, ("a", 7))
         s_qr(7)
         take_words(S, ("g", 7))
         s_r(6)
-        less_g(G, 7)
+        less_g(G, 7, cols(0))
         v_dr(both(5))
         add_dr(G, 5)
         v_dar(both(5))
@@ -494,10 +492,10 @@ def tile_grucell_v_kernel(
         v_daz(7, 0)
         il(V, ("dar", 1, 0))
         take_words(S, ("d", first))
-        il(S, ("in", 0, 0), ("raw", 2))
         v_daz(7, 1)
         pe_d(second, 0)
         qe(("dar", 1, 0))
+        il(S, ("in", 0, 0))
         pe_out1(0, 3)
         pe_out1(1, 2)
         q_dar(both(5))
@@ -520,30 +518,34 @@ def tile_grucell_v_kernel(
             pe_out1(b, ring[b % 4])
         q_dar(first)
         v_dar(second)
-        take_words(S, ("d", second))
-        pe_out1(7, ring[3])
+        out1(S, 4)
+        pe_out1(7, 3)
         qe(("in", 0, 0))
         qe(("in", 1, 0))
-        for b in range(4, 8):
+        out1(S, 5)
+        pe_out1(8, 4)
+        take_words(S, ("d", second))
+        pe_out1(9, 2)
+        for b in range(6, 8):
             out1(S, b)
-            pe_out1(b + 4, ring[b % 4])
-        il(S, ("dar", 0, 1))
+            pe_out1(b + 4, (5, 3)[b - 6])
         il(V, ("dar", 1, 1))
         q_dar(second)
         v_out0(5)
         pe_out0(6)
         qe(("dar", 1, 1))
-        v_dr(second)
         qe(("dar", 0, 1))
+        v_dr(second)
         q_daz(7)
+        less_g(V, 7, cols(1))
         add_dr(V, 6)
-        ring = (0, 1, 3, 4, 5, 2)
+        add_dr(V, 7)
+        ring = (0, 1, 4, 2, 5, 3)
         for b in range(12, 18):
             if b >= 14:
                 out1(S, b - 6)
             pe_out1(b, ring[b % 6])
         v_out0(6)
-        add_dr(V, 7)
         pe_out0(7)
         for b in range(12, 18):
             out1(S, b)

@@ -23,6 +23,7 @@ PACK = 4
 NB = 512
 KP = 2
 TILES = 8
+G_SHARE = 768
 
 SIXTH = 1.0 / 6.0
 EDGE = 1.0 + 2.0 ** -8
@@ -164,9 +165,9 @@ def tile_grucell_v_kernel(
             V.tensor_scalar(out=clip[i][:].rearrange("p s n -> p n s"), in0=ah[i][:].rearrange("p (n s) -> p n s", s=PACK),
                             scalar1=-1.0, scalar2=1.0, op0=ALU.max, op1=ALU.min)
 
-        def pe_e(i):
+        def pe_e(i, first_bank=0):
             for kp in range(KP):
-                e_ps[i, kp] = bank(kp)
+                e_ps[i, kp] = bank(first_bank + kp)
                 for s in range(PACK):
                     for src, first in ((clip, True), (neg_h, False)):
                         PE.matmul(out=e_ps[i, kp][:, cols(s, P)], lhsT=src[i][:, s, cols(kp, P)], rhs=ident[:],
@@ -200,9 +201,9 @@ def tile_grucell_v_kernel(
         def v_mz(i):
             V.tensor_scalar(out=qz[i][:], in0=qz[i][:], scalar1=EDGE, scalar2=None, op0=ALU.is_lt)
 
-        def v_gm(i):
+        def v_gm(i, at_bank=3):
             V.tensor_tensor(out=qz[i][:], in0=qz[i][:], in1=gg[i][:], op=ALU.mult)
-            turn_words(("g", i), [qz[i][:, cols(n)] for n in range(2)], 3)
+            turn_words(("g", i), [qz[i][:, cols(n)] for n in range(2)], at_bank)
 
         def less_g(eng, i, at=slice(0, H)):
             y = term(i)[:, at]
@@ -283,11 +284,14 @@ def tile_grucell_v_kernel(
             for n in range(2):
                 y = terms[i][:, cols(n)]
                 V.tensor_tensor(out=y, in0=o_ps[i, n][:], in1=y, op=ALU.add)
-                Q.dma_start(out=o0_h[:, i // 4, i % 4, cols(n)], in_=y)
+                if i == TILES - 1:
+                    Q.dma_start(out=o0_h[:, i // 4, i % 4, cols(n)], in_=y)
+            if i < TILES - 1:
+                Q.dma_start(out=o0_h[:, i // 4, i % 4, :], in_=term(i))
 
         stage = {}
 
-        blocks = [(m, n) for x in range(2) for n in (1, 2, 0) for m in range(4 * x, 4 * x + 4)]
+        blocks = [(m, n) for n in (1, 2, 0) for m in range(4)] + [(m, n) for m in range(4, 8) for n in range(3)]
 
         def pe_out1(b, at_bank):
             m, n = blocks[b]
@@ -302,11 +306,18 @@ def tile_grucell_v_kernel(
 
         def out1(eng, b):
             m, n = blocks[b]
-            if b % 2 == 0:
-                stage[b // 2] = sb([P, 2, NB], F32, *(("az", 2), ("ah", 2), ("clip", 2))[b // 2 % 3])
-            dst = stage[b // 2][:, b % 2, :]
-            copy(eng, dst, o_ps[b][:])
-            Q.dma_start(out=out_1[cols(m, P), cols(n)], in_=dst)
+            if m < 4:
+                if b % 2 == 0:
+                    stage[b // 2] = sb([P, 2, NB], F32, ("az", "ah", "clip")[b // 2 % 3], 2)
+                dst = stage[b // 2][:, b % 2, :]
+                copy(eng, dst, o_ps[b][:])
+                Q.dma_start(out=out_1[cols(m, P), cols(n)], in_=dst)
+            else:
+                if n == 0:
+                    stage["row", m] = sb([P, C], F32, ("raw", "hnat")[m % 2], 2)
+                copy(eng, stage["row", m][:, cols(n)], o_ps[b][:])
+                if n == 2:
+                    Q.dma_start(out=out_1[cols(m, P), :], in_=stage["row", m][:])
 
         def both(i):
             return ((i, 0), (i, 1))
@@ -398,7 +409,7 @@ def tile_grucell_v_kernel(
 
         extra = {
             2: ((S, ("z", 0, 1)), (V, ("z", 1, 0)), (S, ("z", 1, 1))),
-            3: ((S, ("r", 0, 1)), (V, ("r", 0, 0)), (S, ("r", 1, 0))),
+            3: ((V, ("r", 0, 0)), (S, ("r", 0, 1)), (S, ("r", 1, 0))),
             4: (),
             5: ((S, ("hp", 0, 0)),),
             6: ((S, ("hp", 1, 0)),),
@@ -427,9 +438,13 @@ def tile_grucell_v_kernel(
             take_words(S, ("g", k))
             negate_h(S, k + 1)
             if k >= 4:
-                less_g(G, k, cols(0))
+                less_g(G, k, slice(0, G_SHARE))
             v_dr(both(b))
-            add_dr(G, b)
+            if k < 4:
+                add_dr(G, b, cols(0))
+                add_dr(G, b, cols(1))
+            else:
+                add_dr(G, b)
             v_dar(both(b))
             load_ar(b + 3)
             daz(k - 1)
@@ -438,7 +453,7 @@ def tile_grucell_v_kernel(
             pe_d(both(b + 1))
             pe_e(k)
             take_words(S, ("d", both(b)))
-            less_g(V, k, cols(1) if k >= 4 else slice(0, H))
+            less_g(V, k, slice(G_SHARE if k >= 4 else 0, H))
             if k + 3 < TILES:
                 load_g(k + 3)
             v_mr(b + 1)
@@ -447,14 +462,17 @@ def tile_grucell_v_kernel(
             waiting = []
             if b > 0:
                 q_dar(both(b - 1))
+            if k == 3:
+                il(V, ("r", 0, 0))
             v_hm(b + 1)
             for eng, key in extra[k]:
-                il(eng, key)
+                if key != ("r", 0, 0):
+                    il(eng, key)
                 if key != ("r", 1, 0):
                     waiting.append(key)
                 if key[2] == 1 and key[0] == "z":
                     load_w("r", key[1])
-                if key == ("r", 0, 0):
+                if key == ("r", 0, 1):
                     load_inputs()
             if k >= 4:
                 pe_out0(k - 3)
@@ -467,7 +485,7 @@ def tile_grucell_v_kernel(
         s_qr(7)
         take_words(S, ("g", 7))
         s_r(6)
-        less_g(G, 7, cols(0))
+        less_g(G, 7, slice(0, G_SHARE))
         v_dr(both(5))
         add_dr(G, 5)
         v_dar(both(5))
@@ -518,7 +536,7 @@ def tile_grucell_v_kernel(
             pe_out1(b, ring[b % 4])
         q_dar(first)
         v_dar(second)
-        out1(S, 4)
+        out1(V, 4)
         pe_out1(7, 3)
         qe(("in", 0, 0))
         qe(("in", 1, 0))
@@ -530,26 +548,27 @@ def tile_grucell_v_kernel(
             out1(S, b)
             pe_out1(b + 4, (5, 3)[b - 6])
         il(V, ("dar", 1, 1))
-        q_dar(second)
-        v_out0(5)
-        pe_out0(6)
-        qe(("dar", 1, 1))
         qe(("dar", 0, 1))
-        v_dr(second)
-        q_daz(7)
-        less_g(V, 7, cols(1))
-        add_dr(V, 6)
-        add_dr(V, 7)
-        ring = (0, 1, 4, 2, 5, 3)
-        for b in range(12, 18):
-            if b >= 14:
-                out1(S, b - 6)
-            pe_out1(b, ring[b % 6])
-        v_out0(6)
-        pe_out0(7)
-        for b in range(12, 18):
+        q_dar(second)
+        qe(("dar", 1, 1))
+        ring = (4, 2, 5, 3, 0, 1)
+        for b in range(8, 12):
             out1(S, b)
+            pe_out1(b + 4, ring[(b + 4) % 6])
+        v_dr(second)
+        add_dr(G, 6)
+        v_out0(5)
+        for b in range(16, 18):
+            pe_out1(b, ring[b % 6])
+        for b in range(12, 18):
+            out1(V if b == 12 else S, b)
             pe_out1(b + 6, ring[b % 6])
-        v_out0(7)
+        less_g(V, 7, slice(G_SHARE, H))
+        q_daz(7)
+        pe_out0(6)
+        add_dr(V, 7)
         for b in range(18, 24):
-            out1(V if b % 2 else S, b)
+            out1(V if b < 20 else S, b)
+        pe_out0(7, 4)
+        v_out0(6)
+        v_out0(7)

@@ -23,7 +23,7 @@ PACK = 4
 NB = 512
 KP = 2
 TILES = 8
-G_SHARE = 768
+G_SHARE = 640
 
 SIXTH = 1.0 / 6.0
 EDGE = 1.0 + 2.0 ** -8
@@ -58,7 +58,7 @@ def tile_grucell_v_kernel(
         def cols(n, width=NB):
             return slice(n * width, (n + 1) * width)
 
-        half = sb([P, 1], F32, "half")
+        seed, half = sb([P, 1], F32, "seed"), sb([P, 1], F32, "half")
         ident = sb([P, P], F32, "ident")
 
         w_scales = {n: sb([P, KP, H], U8, "ws" + n) for n in "hzr"}
@@ -110,15 +110,16 @@ def tile_grucell_v_kernel(
             else:
                 V.tensor_copy(out=dst, in_=src)
 
-        def il(eng, key, tag=("grouped", 3)):
+        def il(eng, key, tag=("grouped", 3), lo=0, hi=NB):
             name, g, n = key
-            grouped[key] = sb([P, NB * PACK], BF16, *tag)
+            if lo == 0:
+                grouped[key] = sb([P, NB * PACK], BF16, *tag)
             if name == "in":
                 src = raw["in"][:, g]
             else:
                 src = {"hp": h_nat, "dar": dar}[name][g] if name in ("hp", "dar") else raw[name, g]
                 src = src[:, :, cols(n)]
-            interleave(eng, grouped[key][:], src)
+            interleave(eng, grouped[key][:, lo * PACK:hi * PACK], src[:, :, lo:hi])
 
         def qe(key):
             name, g, n = key
@@ -354,7 +355,8 @@ def tile_grucell_v_kernel(
         load_w("h", 0)
         load_h(0, 1, 2)
         load_w("h", 1)
-        V.memset(half[:], 0.5)
+        V.memset(seed[:], 0.5)
+        S.activation(out=half[:], in_=seed[:], func=ACT.Relu)
         make_identity(nc, ident[:])
         s_p(0)
         s_qh(0)
@@ -381,7 +383,8 @@ def tile_grucell_v_kernel(
         qe(("h", 0, 0))
         il(S, ("h", 1, 0))
         qe(("h", 0, 1))
-        il(V, ("h", 1, 1))
+        il(V, ("h", 1, 1), hi=NB // 2)
+        il(S, ("h", 1, 1), lo=NB // 2)
 
         front(1)
         load_w("z", 1)
@@ -435,7 +438,8 @@ def tile_grucell_v_kernel(
                 pe_out0(0)
             take_words(S, ("a", k))
             s_r(b + 1)
-            take_words(S, ("g", k))
+            if k >= 4:
+                take_words(S, ("g", k))
             negate_h(S, k + 1)
             if k >= 4:
                 less_g(G, k, slice(0, G_SHARE))
@@ -450,6 +454,8 @@ def tile_grucell_v_kernel(
             daz(k - 1)
             if k >= 4:
                 v_out0(k - 4)
+            else:
+                take_words(V, ("g", k))
             pe_d(both(b + 1))
             pe_e(k)
             take_words(S, ("d", both(b)))

@@ -70,9 +70,10 @@ def tile_grucell_v_kernel(
         qh, qz, clip, neg_h, e_ps, dz2_t, gm_t, daz_t, words_ps = {}, {}, {}, {}, {}, {}, {}, {}, {}
         ar, dar, d_ps, dar_t, o_ps, dz2_q, daz_q, dar_q = {}, {}, {}, {}, {}, {}, {}, {}
 
-        def load_az(i):
-            az[i] = sb([P, H], F32, "az", 2)
-            Q.dma_start(out=az[i][:], in_=az_h[:, i // 4, i % 4, :])
+        def load_az(i, at=slice(0, H)):
+            if at.start == 0:
+                az[i] = sb([P, H], F32, "az", 2)
+            Q.dma_start(out=az[i][:, at], in_=az_h[:, i // 4, i % 4, at])
 
         def load_ah(i):
             ah[i] = sb([P, H], F32, "ah", 2)
@@ -87,9 +88,10 @@ def tile_grucell_v_kernel(
                 h_nat[g] = sb([P, PACK, H], BF16, "hnat", 2)
             Q.dma_start(out=h_nat[g][:, t0:t1, :], in_=h_h[:, g, t0:t1, :])
 
-        def load_w(n, kp):
-            raw[n, kp] = sb([P, PACK, H], BF16, "raw", 2)
-            Q.dma_start(out=raw[n, kp][:], in_=w_h[n][:, kp])
+        def load_w(n, kp, at=slice(0, H)):
+            if at.start == 0:
+                raw[n, kp] = sb([P, PACK, H], BF16, "raw", 2)
+            Q.dma_start(out=raw[n, kp][:, :, at], in_=w_h[n][:, kp, :, at])
 
         def load_inputs():
             raw["in"] = sb([P, KP, PACK, I], BF16, "raw", 2)
@@ -140,17 +142,19 @@ def tile_grucell_v_kernel(
         def term(i):
             return terms[i][:]
 
-        def s_p(i):
-            terms[i] = sb([P, H], F32, "terms", 7)
-            S.activation(out=term(i), in_=az[i][:], func=ACT.Relu, bias=half[:], scale=-SIXTH)
+        def s_p(i, at=slice(0, H)):
+            if at.start == 0:
+                terms[i] = sb([P, H], F32, "terms", 7)
+            S.activation(out=term(i)[:, at], in_=az[i][:, at], func=ACT.Relu, bias=half[:], scale=-SIXTH)
 
         def s_qh(i):
             qh[i] = sb([P, H], BF16, "qh", 2)
             S.activation(out=qh[i][:], in_=ah[i][:], func=ACT.Square, scale=ROOT_1)
 
-        def s_qz(i):
-            qz[i] = sb([P, H], BF16, "qz", 2)
-            S.activation(out=qz[i][:], in_=az[i][:], func=ACT.Square, scale=ROOT_3)
+        def s_qz(i, at=slice(0, H)):
+            if at.start == 0:
+                qz[i] = sb([P, H], BF16, "qz", 2)
+            S.activation(out=qz[i][:, at], in_=az[i][:, at], func=ACT.Square, scale=ROOT_3)
 
         def negate_h(eng, i):
             neg_h[i] = sb([P, PACK, KP * P], F32, "negh", 2)
@@ -192,15 +196,16 @@ def tile_grucell_v_kernel(
             copy(eng, out[:].bitcast(F32), words_ps[key][:].rearrange("p (k u r) -> p k r u", k=KP, u=2))
             {"a": dz2_t, "g": gm_t, "d": dar_t}[key[0]][key[1]] = out
 
-        def v_u(i):
-            V.scalar_tensor_tensor(out=term(i), in0=term(i), scalar=1.0, in1=gg[i][:], op0=ALU.min, op1=ALU.mult)
+        def v_u(i, at=slice(0, H)):
+            y = term(i)[:, at]
+            V.scalar_tensor_tensor(out=y, in0=y, scalar=1.0, in1=gg[i][:, at], op0=ALU.min, op1=ALU.mult)
 
         def v_dz2(i):
             V.scalar_tensor_tensor(out=qh[i][:], in0=qh[i][:], scalar=EDGE, in1=term(i), op0=ALU.is_lt, op1=ALU.mult)
             turn_words(("a", i), [qh[i][:, cols(n)] for n in range(2)], 2)
 
-        def v_mz(i):
-            V.tensor_scalar(out=qz[i][:], in0=qz[i][:], scalar1=EDGE, scalar2=None, op0=ALU.is_lt)
+        def v_mz(i, at=slice(0, H)):
+            V.tensor_scalar(out=qz[i][:, at], in0=qz[i][:, at], scalar1=EDGE, scalar2=None, op0=ALU.is_lt)
 
         def v_gm(i, at_bank=3):
             V.tensor_tensor(out=qz[i][:], in0=qz[i][:], in1=gg[i][:], op=ALU.mult)
@@ -328,8 +333,6 @@ def tile_grucell_v_kernel(
             if k + 2 < TILES:
                 load_ah(k + 2)
             v_u(k)
-            if k == 0:
-                negate_h(V, 0)
             v_mz(k)
             if k > 0:
                 q_dz2(k - 1)
@@ -351,9 +354,11 @@ def tile_grucell_v_kernel(
         load_g(0)
         load_h(0, 0, 1)
         load_az(1)
-        load_ah(1)
         load_w("h", 0)
+        load_ah(1)
         load_h(0, 1, 2)
+        load_g(1)
+        load_ar(0)
         load_w("h", 1)
         V.memset(seed[:], 0.5)
         S.activation(out=half[:], in_=seed[:], func=ACT.Relu)
@@ -362,42 +367,45 @@ def tile_grucell_v_kernel(
         s_qh(0)
         s_qz(0)
         load_az(2)
-        load_g(1)
-
-        front(0)
+        v_clip(0)
+        load_ah(2)
+        v_u(0)
+        negate_h(V, 0)
+        v_mz(0)
+        v_dz2(0)
+        v_gm(0)
         pe_e(0)
-        load_ar(0)
-        load_h(0, 2, PACK)
+        load_g(2)
         s_p(1)
-        s_qh(1)
         s_qz(1)
-        negate_h(S, 1)
         turned(0)
+        s_qh(1)
+        negate_h(S, 1)
         less_g(V, 0)
         il(V, ("h", 0, 0))
         il(V, ("h", 0, 1))
+        qe(("h", 0, 0))
+        qe(("h", 0, 1))
         load_w("z", 0)
+        load_h(0, 2, PACK)
         load_ar(1)
         load_az(3)
-        load_g(2)
-        qe(("h", 0, 0))
+        s_qr(0)
+        s_r(0)
         il(S, ("h", 1, 0))
-        qe(("h", 0, 1))
-        il(V, ("h", 1, 1), hi=NB // 2)
-        il(S, ("h", 1, 1), lo=NB // 2)
 
         front(1)
+        daz(0)
+        il(V, ("h", 1, 1))
         load_w("z", 1)
         load_g(3)
         s_p(2)
         s_qh(2)
         s_qz(2)
         load_az(4)
-        s_qr(0)
-        il(S, ("z", 0, 0))
         turned(1)
+        il(S, ("z", 0, 0))
         negate_h(S, 2)
-        daz(0)
         pe_e(1)
         qe(("h", 1, 0))
         less_g(V, 1)
@@ -405,7 +413,6 @@ def tile_grucell_v_kernel(
         v_mr(0)
         qe(("h", 1, 1))
         pe_d(both(0))
-        s_r(0)
         v_hm(0)
         load_ar(2)
         load_h(1, 0, PACK)

@@ -23,7 +23,7 @@ PACK = 4
 NB = 512
 KP = 2
 TILES = 8
-G_SHARE = 640
+G_SHARE = 768
 
 SIXTH = 1.0 / 6.0
 EDGE = 1.0 + 2.0 ** -8

@@ -23,7 +23,8 @@ PACK = 4
 NB = 512
 KP = 2
 TILES = 8
-G_SHARE = 768
+G_SHARE = 896
+G_EARLY = 320
 
 SIXTH = 1.0 / 6.0
 EDGE = 1.0 + 2.0 ** -8
@@ -448,8 +449,8 @@ def tile_grucell_v_kernel(
             if k >= 4:
                 take_words(S, ("g", k))
             negate_h(S, k + 1)
-            if k >= 4:
-                less_g(G, k, slice(0, G_SHARE))
+            share = G_SHARE if k >= 4 else G_EARLY
+            less_g(G, k, slice(0, share))
             v_dr(both(b))
             if k < 4:
                 add_dr(G, b, cols(0))
@@ -466,7 +467,7 @@ def tile_grucell_v_kernel(
             pe_d(both(b + 1))
             pe_e(k)
             take_words(S, ("d", both(b)))
-            less_g(V, k, slice(G_SHARE if k >= 4 else 0, H))
+            less_g(V, k, slice(share, H))
             if k + 3 < TILES:
                 load_g(k + 3)
             v_mr(b + 1)

@@ -24,7 +24,8 @@ NB = 512
 KP = 2
 TILES = 8
 G_SHARE = 896
-G_EARLY = 320
+G_EARLY = 640
+G_FIRST = 384
 
 SIXTH = 1.0 / 6.0
 EDGE = 1.0 + 2.0 ** -8
@@ -68,6 +69,8 @@ def tile_grucell_v_kernel(
         tok_codes, tok_scales = sb([P, KP, H], U32, "tokc"), sb([P, KP, H], U8, "toks")
 
         az, ah, gg, raw, h_nat, terms, grouped = {}, {}, {}, {}, {}, {}, {}
+
+        pair = {}
         qh, qz, clip, neg_h, e_ps, dz2_t, gm_t, daz_t, words_ps = {}, {}, {}, {}, {}, {}, {}, {}, {}
         ar, dar, d_ps, dar_t, o_ps, dz2_q, daz_q, dar_q = {}, {}, {}, {}, {}, {}, {}, {}
 
@@ -134,6 +137,18 @@ def tile_grucell_v_kernel(
             else:
                 quant(w_codes[name][:, g, cols(n)], w_scales[name][:, g, cols(n)], grouped[key][:], E4M3X4)
 
+        def pair_half(j, which):
+            if j not in pair:
+                pair[j] = sb([P, 2, KP, P, PACK], BF16, "pair", 2)
+            return pair[j][:, which]
+
+        def q_pair(j, which=slice(0, 2)):
+            codes, scales = sb([P, 2, KP, P], U32, "pairc", 5), sb([P, 2, KP, P], U8, "pairs", 5)
+            quant(codes[:, which].rearrange("p w k r -> p (w k r)"), scales[:, which].rearrange("p w k r -> p (w k r)"),
+                  pair[j][:, which].rearrange("p w k r s -> p (w k r s)"), E5M2X4)
+            for w in range(which.start, which.stop):
+                (dz2_q, daz_q)[w][j - w] = [(codes[:, w, k], scales[:, w, k]) for k in range(KP)]
+
         def quant_turned(tag, bufs, src):
             codes, scales = sb([P, 2, P], U32, tag + "c", bufs), sb([P, 2, P], U8, tag + "s", bufs)
             quant(codes[:].rearrange("p k r -> p (k r)"), scales[:].rearrange("p k r -> p (k r)"),
@@ -193,9 +208,12 @@ def tile_grucell_v_kernel(
                 V.tensor_copy(out=dst, in_=src)
 
         def take_words(eng, key):
-            out = sb([P, KP, P, PACK], BF16, "turned" + key[0], 2)
-            copy(eng, out[:].bitcast(F32), words_ps[key][:].rearrange("p (k u r) -> p k r u", k=KP, u=2))
-            {"a": dz2_t, "g": gm_t, "d": dar_t}[key[0]][key[1]] = out
+            if key[0] == "a":
+                out = pair_half(key[1], 0)
+            else:
+                out = sb([P, KP, P, PACK], BF16, "turned" + key[0], 2)[:]
+                {"g": gm_t, "d": dar_t}[key[0]][key[1]] = out
+            copy(eng, out.bitcast(F32), words_ps[key][:].rearrange("p (k u r) -> p k r u", k=KP, u=2))
 
         def v_u(i, at=slice(0, H)):
             y = term(i)[:, at]
@@ -217,16 +235,8 @@ def tile_grucell_v_kernel(
             eng.tensor_tensor(out=y, in0=y, in1=gg[i][:, at], op=ALU.subtract)
 
         def v_daz(i, kp):
-            if kp == 0:
-                daz_t[i] = sb([P, KP, P, PACK], BF16, "daz")
-            V.scalar_tensor_tensor(out=daz_t[i][:, kp], in0=e_ps[i, kp][:].rearrange("p (s r) -> p r s", s=PACK),
+            V.scalar_tensor_tensor(out=pair_half(i + 1, 1)[:, kp], in0=e_ps[i, kp][:].rearrange("p (s r) -> p r s", s=PACK),
                                    scalar=-SIXTH, in1=gm_t[i][:, kp], op0=ALU.mult, op1=ALU.mult)
-
-        def q_dz2(i):
-            dz2_q[i] = quant_turned("dz2", 3, dz2_t[i])
-
-        def q_daz(i):
-            daz_q[i] = quant_turned("dazq", 4, daz_t[i])
 
         def s_qr(i, at=slice(0, H)):
             if i % 4 == 0:
@@ -335,11 +345,8 @@ def tile_grucell_v_kernel(
                 load_ah(k + 2)
             v_u(k)
             v_mz(k)
-            if k > 0:
-                q_dz2(k - 1)
+            q_pair(k - 1, slice(0, 2 if k > 1 else 1))
             v_dz2(k)
-            if k > 1:
-                q_daz(k - 2)
             v_gm(k)
 
         def turned(k):
@@ -396,6 +403,7 @@ def tile_grucell_v_kernel(
         il(S, ("h", 1, 0))
 
         front(1)
+        less_g(G, 1, slice(0, G_FIRST))
         daz(0)
         il(V, ("h", 1, 1))
         load_w("z", 1)
@@ -409,7 +417,7 @@ def tile_grucell_v_kernel(
         negate_h(S, 2)
         pe_e(1)
         qe(("h", 1, 0))
-        less_g(V, 1)
+        less_g(V, 1, slice(G_FIRST, H))
         load_g(4)
         v_mr(0)
         qe(("h", 1, 1))
@@ -452,11 +460,7 @@ def tile_grucell_v_kernel(
             share = G_SHARE if k >= 4 else G_EARLY
             less_g(G, k, slice(0, share))
             v_dr(both(b))
-            if k < 4:
-                add_dr(G, b, cols(0))
-                add_dr(G, b, cols(1))
-            else:
-                add_dr(G, b)
+            add_dr(G, b)
             v_dar(both(b))
             load_ar(b + 3)
             daz(k - 1)
@@ -505,7 +509,7 @@ def tile_grucell_v_kernel(
         v_dar(both(5))
         daz(6)
         v_out0(3)
-        q_dz2(7)
+        q_pair(7, slice(0, 1))
         pe_d(first)
         pe_e(7)
         take_words(S, ("d", both(5)))
@@ -517,7 +521,7 @@ def tile_grucell_v_kernel(
         q_dar(both(4))
         v_hm(6, 2, cols(0))
         pe_out0(4)
-        q_daz(6)
+        q_pair(7, slice(1, 2))
 
         s_r(7)
         v_dar(first)
@@ -578,7 +582,7 @@ def tile_grucell_v_kernel(
             out1(V if b == 12 else S, b)
             pe_out1(b + 6, ring[b % 6])
         less_g(V, 7, slice(G_SHARE, H))
-        q_daz(7)
+        q_pair(8, slice(1, 2))
         pe_out0(6)
         add_dr(V, 7)
         for b in range(18, 24):

@@ -26,6 +26,7 @@ TILES = 8
 G_SHARE = 896
 G_EARLY = 640
 G_FIRST = 384
+V_LAST = 256
 
 SIXTH = 1.0 / 6.0
 EDGE = 1.0 + 2.0 ** -8
@@ -172,14 +173,10 @@ def tile_grucell_v_kernel(
                 qz[i] = sb([P, H], BF16, "qz", 2)
             S.activation(out=qz[i][:, at], in_=az[i][:, at], func=ACT.Square, scale=ROOT_3)
 
-        def negate_h(eng, i):
+        def s_negate_h(i):
             neg_h[i] = sb([P, PACK, KP * P], F32, "negh", 2)
-            dst = neg_h[i][:].rearrange("p s (b e) -> p b s e", e=4)
-            src = h_nat[i // 4][:, i % 4, :].rearrange("p (b e s) -> p b s e", e=4, s=PACK)
-            if eng is S:
-                S.activation(out=dst, in_=src, func=ACT.Copy, scale=-1.0)
-            else:
-                V.tensor_scalar(out=dst, in0=src, scalar1=-1.0, scalar2=None, op0=ALU.mult)
+            S.activation(out=neg_h[i][:].rearrange("p s (b e) -> p b s e", e=4),
+                         in_=h_nat[i // 4][:, i % 4, :].rearrange("p (b e s) -> p b s e", e=4, s=PACK), func=ACT.Copy, scale=-1.0)
 
         def v_clip(i):
             clip[i] = sb([P, PACK, KP * P], F32, "clip", 2)
@@ -378,18 +375,18 @@ def tile_grucell_v_kernel(
         v_clip(0)
         load_ah(2)
         v_u(0)
-        negate_h(V, 0)
-        v_mz(0)
         v_dz2(0)
+        v_mz(0)
+        less_g(V, 0)
         v_gm(0)
-        pe_e(0)
         load_g(2)
         s_p(1)
         s_qz(1)
+        s_negate_h(0)
+        pe_e(0)
         turned(0)
         s_qh(1)
-        negate_h(S, 1)
-        less_g(V, 0)
+        s_negate_h(1)
         il(V, ("h", 0, 0))
         il(V, ("h", 0, 1))
         qe(("h", 0, 0))
@@ -414,7 +411,7 @@ def tile_grucell_v_kernel(
         load_az(4)
         turned(1)
         il(S, ("z", 0, 0))
-        negate_h(S, 2)
+        s_negate_h(2)
         pe_e(1)
         qe(("h", 1, 0))
         less_g(V, 1, slice(G_FIRST, H))
@@ -439,7 +436,7 @@ def tile_grucell_v_kernel(
             b = k - 2
             if k == 4:
                 qe(waiting.pop(0))
-                il(S, ("r", 1, 1))
+                il(S, ("r", 1, 1), hi=NB - V_LAST)
             s_qr(b + 1)
             s_p(k + 1)
             s_qh(k + 1)
@@ -448,6 +445,7 @@ def tile_grucell_v_kernel(
                 load_az(k + 3)
             front(k)
             if k == 4:
+                il(V, ("r", 1, 1), lo=NB - V_LAST)
                 qe(waiting.pop(0))
                 qe(("r", 1, 0))
                 qe(("r", 1, 1))
@@ -456,7 +454,7 @@ def tile_grucell_v_kernel(
             s_r(b + 1)
             if k >= 4:
                 take_words(S, ("g", k))
-            negate_h(S, k + 1)
+            s_negate_h(k + 1)
             share = G_SHARE if k >= 4 else G_EARLY
             less_g(G, k, slice(0, share))
             v_dr(both(b))
@@ -557,6 +555,7 @@ def tile_grucell_v_kernel(
         out1(V, 4)
         pe_out1(7, 3)
         qe(("in", 0, 0))
+        qe(("dar", 0, 1))
         qe(("in", 1, 0))
         out1(S, 5)
         pe_out1(8, 4)
@@ -566,7 +565,6 @@ def tile_grucell_v_kernel(
             out1(S, b)
             pe_out1(b + 4, (5, 3)[b - 6])
         il(V, ("dar", 1, 1))
-        qe(("dar", 0, 1))
         q_dar(second)
         qe(("dar", 1, 1))
         ring = (4, 2, 5, 3, 0, 1)

@@ -27,6 +27,7 @@ G_SHARE = 896
 G_EARLY = 640
 G_FIRST = 384
 V_LAST = 256
+CATCH = 6
 
 SIXTH = 1.0 / 6.0
 EDGE = 1.0 + 2.0 ** -8
@@ -251,9 +252,9 @@ def tile_grucell_v_kernel(
             y = dar[i // 4][:, i % 4:i % 4 + tiles, at]
             V.tensor_tensor(out=y, in0=y, in1=h_nat[i // 4][:, i % 4:i % 4 + tiles, at], op=ALU.mult)
 
-        def pe_d(units, first_bank=4):
-            for b, (i, n) in enumerate(units):
-                d_ps[i, n] = bank(first_bank + b)
+        def pe_d(units, banks=(4, 5)):
+            for (i, n), at_bank in zip(units, banks):
+                d_ps[i, n] = bank(at_bank)
                 for kp in range(KP):
                     codes, scales = dz2_q[i][kp]
                     PE.matmul_mx(
@@ -281,9 +282,9 @@ def tile_grucell_v_kernel(
             for unit, operand in zip(units, quant_turned("darq", 4, dar_t[units])):
                 dar_q[unit] = operand
 
-        def pe_out0(i, first_bank=6):
-            for n in range(2):
-                o_ps[i, n] = bank(first_bank + n)
+        def pe_out0(i, banks=(6, 7), only=None):
+            for n in range(2) if only is None else (only - 1,):
+                o_ps[i, n] = bank(banks[n])
                 for k in range(2 * KP):
                     kp = k % KP
                     codes, scales = daz_q[i][kp] if k < KP else dar_q[i, kp]
@@ -305,7 +306,8 @@ def tile_grucell_v_kernel(
 
         stage = {}
 
-        blocks = [(m, n) for n in (1, 2, 0) for m in range(4)] + [(m, n) for m in range(4, 8) for n in range(3)]
+        blocks = ([(m, n) for n in (1, 2) for m in range(4)] + [(m, n) for m in range(4, 8) for n in (1, 2)]
+                  + [(m, 0) for m in range(8)])
 
         def pe_out1(b, at_bank):
             m, n = blocks[b]
@@ -320,24 +322,28 @@ def tile_grucell_v_kernel(
 
         def out1(eng, b):
             m, n = blocks[b]
-            if m < 4:
+            if m < 4 or n == 0:
                 if b % 2 == 0:
-                    stage[b // 2] = sb([P, 2, NB], F32, ("az", "ah", "clip")[b // 2 % 3], 2)
+                    stage[b // 2] = sb([P, 2, NB], F32, ("az", "ah", "clip", "negh")[b // 2 % 4], 2)
                 dst = stage[b // 2][:, b % 2, :]
                 copy(eng, dst, o_ps[b][:])
                 Q.dma_start(out=out_1[cols(m, P), cols(n)], in_=dst)
             else:
-                if n == 0:
-                    stage["row", m] = sb([P, C], F32, ("raw", "hnat")[m % 2], 2)
-                copy(eng, stage["row", m][:, cols(n)], o_ps[b][:])
+                if n == 1:
+                    stage["row", m] = sb([P, 2 * NB], F32, "terms", 7)
+                copy(eng, stage["row", m][:, cols(n - 1)], o_ps[b][:])
                 if n == 2:
-                    Q.dma_start(out=out_1[cols(m, P), :], in_=stage["row", m][:])
+                    Q.dma_start(out=out_1[cols(m, P), NB:], in_=stage["row", m][:])
 
         def both(i):
             return ((i, 0), (i, 1))
 
-        def front(k):
+        def front(k, words=False, passes=False):
             v_clip(k)
+            if words:
+                q_dar(both(k - 3))
+            if passes:
+                pe_out0(k - 3, only=1)
             if k + 2 < TILES:
                 load_ah(k + 2)
             v_u(k)
@@ -443,7 +449,7 @@ def tile_grucell_v_kernel(
             s_qz(k + 1)
             if k + 3 < TILES:
                 load_az(k + 3)
-            front(k)
+            front(k, k >= CATCH, k > CATCH)
             if k == 4:
                 il(V, ("r", 1, 1), lo=NB - V_LAST)
                 qe(waiting.pop(0))
@@ -457,13 +463,16 @@ def tile_grucell_v_kernel(
             s_negate_h(k + 1)
             share = G_SHARE if k >= 4 else G_EARLY
             less_g(G, k, slice(0, share))
+            if k == CATCH:
+                v_out0(k - 4)
+                pe_out0(k - 3)
             v_dr(both(b))
             add_dr(G, b)
             v_dar(both(b))
             load_ar(b + 3)
             daz(k - 1)
             if k >= 4:
-                v_out0(k - 4)
+                v_out0(k - 4 if k < CATCH else k - 3)
             else:
                 take_words(V, ("g", k))
             pe_d(both(b + 1))
@@ -476,7 +485,7 @@ def tile_grucell_v_kernel(
             for key in waiting:
                 qe(key)
             waiting = []
-            if b > 0:
+            if 0 < b < CATCH - 2:
                 q_dar(both(b - 1))
             if k == 3:
                 il(V, ("r", 0, 0))
@@ -490,101 +499,96 @@ def tile_grucell_v_kernel(
                     load_w("r", key[1])
                 if key == ("r", 0, 1):
                     load_inputs()
-            if k >= 4:
+            if 4 <= k < CATCH:
                 pe_out0(k - 3)
 
         s_qr(6)
         il(S, ("dar", 0, 0))
-        il(S, ("dar", 0, 1), ("raw", 2))
-        front(7)
+        il(S, ("hp", 0, 1), ("raw", 2))
+        front(7, True, True)
+        pe_out0(4, only=2)
         take_words(S, ("a", 7))
         s_qr(7)
         take_words(S, ("g", 7))
-        s_r(6)
         less_g(G, 7, slice(0, G_SHARE))
         v_dr(both(5))
         add_dr(G, 5)
         v_dar(both(5))
+        pe_d(both(6))
         daz(6)
-        v_out0(3)
-        q_pair(7, slice(0, 1))
-        pe_d(first)
         pe_e(7)
+        v_out0(4)
+        q_pair(7, slice(0, 1))
+        pe_d(first[1:], (3,))
         take_words(S, ("d", both(5)))
         qe(("hp", 1, 0))
-        il(S, ("hp", 0, 1))
+        il(S, ("hp", 1, 1))
         v_mr(6, 2, cols(0))
         qe(("dar", 0, 0))
-        il(S, ("hp", 1, 1))
-        q_dar(both(4))
+        il(S, ("dar", 0, 1))
+        q_dar(both(5))
         v_hm(6, 2, cols(0))
-        pe_out0(4)
+        pe_out0(5)
         q_pair(7, slice(1, 2))
 
-        s_r(7)
+        s_r(6)
         v_dar(first)
         v_daz(7, 0)
         il(V, ("dar", 1, 0))
         take_words(S, ("d", first))
         v_daz(7, 1)
-        pe_d(second, 0)
+        pe_d(second[1:], (0,))
         qe(("dar", 1, 0))
-        il(S, ("in", 0, 0))
-        pe_out1(0, 3)
-        pe_out1(1, 2)
-        q_dar(both(5))
-        v_dr(first)
-        pe_out1(2, 4)
-        pe_out1(3, 5)
-        v_out0(4)
-        pe_out0(5)
-        out1(S, 0)
-        out1(S, 1)
+        s_r(7)
+        ring = (1, 2, 6, 7)
+        pe_out1(0, ring[0])
+        pe_out1(1, ring[1])
+        v_out0(5)
+        pe_out1(2, ring[2])
+        pe_out1(3, ring[3])
         qe(("hp", 0, 1))
-        out1(S, 2)
-        out1(S, 3)
-        il(S, ("in", 1, 0))
-        v_mr(6, 2, cols(1))
         qe(("hp", 1, 1))
-        v_hm(6, 2, cols(1))
-        ring = (3, 4, 5, 2)
-        for b in range(4, 7):
-            pe_out1(b, ring[b % 4])
-        q_dar(first)
-        v_dar(second)
-        out1(V, 4)
-        pe_out1(7, 3)
-        qe(("in", 0, 0))
-        qe(("dar", 0, 1))
-        qe(("in", 1, 0))
-        out1(S, 5)
-        pe_out1(8, 4)
-        take_words(S, ("d", second))
-        pe_out1(9, 2)
-        for b in range(6, 8):
+        for b in range(4):
             out1(S, b)
-            pe_out1(b + 4, (5, 3)[b - 6])
+            pe_out1(b + 4, ring[b])
+        v_mr(6, 2, cols(1))
+        q_dar(first)
+        v_hm(6, 2, cols(1))
+        v_dr(first[:1])
+        v_dar(second, 4)
+        for b in range(4, 7):
+            out1(S, b)
+        take_words(S, ("d", second))
+        out1(S, 7)
+        qe(("dar", 0, 1))
         il(V, ("dar", 1, 1))
         q_dar(second)
+        pe_out0(6, (4, 5), 1)
         qe(("dar", 1, 1))
-        ring = (4, 2, 5, 3, 0, 1)
-        for b in range(8, 12):
-            out1(S, b)
-            pe_out1(b + 4, ring[(b + 4) % 6])
-        v_dr(second)
+        v_dr(second[:1])
         add_dr(G, 6)
-        v_out0(5)
-        for b in range(16, 18):
-            pe_out1(b, ring[b % 6])
-        for b in range(12, 18):
-            out1(V if b == 12 else S, b)
-            pe_out1(b + 6, ring[b % 6])
+        for b in range(8, 12):
+            pe_out1(b, ring[b % 4])
+        pe_out0(6, (4, 5), 2)
+        il(S, ("in", 0, 0))
+        il(S, ("in", 1, 0))
+        for b in range(8, 12):
+            out1(V, b)
+            pe_out1(b + 4, ring[b % 4])
+        v_out0(6)
+        qe(("in", 0, 0))
+        qe(("in", 1, 0))
         less_g(V, 7, slice(G_SHARE, H))
         q_pair(8, slice(1, 2))
-        pe_out0(6)
-        add_dr(V, 7)
-        for b in range(18, 24):
-            out1(V if b < 20 else S, b)
-        pe_out0(7, 4)
-        v_out0(6)
+        for b in range(12, 16):
+            out1(S, b)
+            pe_out1(b + 4, ring[b % 4])
+        v_dr(both(7))
+        add_dr(G, 7)
+        for b in range(16, 20):
+            out1(V if b == 19 else S, b)
+            pe_out1(b + 4, ring[b % 4])
+        pe_out0(7, (3, 0))
+        for b in range(20, 24):
+            out1(V if b % 2 else S, b)
         v_out0(7)

@@ -27,6 +27,7 @@ G_SHARE = 896
 G_EARLY = 640
 G_FIRST = 384
 V_LAST = 256
+S_INPUTS = 192
 CATCH = 6
 
 SIXTH = 1.0 / 6.0
@@ -129,10 +130,11 @@ def tile_grucell_v_kernel(
                 src = src[:, :, cols(n)]
             interleave(eng, grouped[key][:, lo * PACK:hi * PACK], src[:, :, lo:hi])
 
-        def qe(key):
+        def qe(key, lo=0, hi=NB):
             name, g, n = key
             if name == "dar":
-                quant(tok_codes[:, g, cols(n)], tok_scales[:, g, cols(n)], grouped[key][:], E5M2X4)
+                at = slice(n * NB + lo, n * NB + hi)
+                quant(tok_codes[:, g, at], tok_scales[:, g, at], grouped[key][:, lo * PACK:hi * PACK], E5M2X4)
             elif name in ("in", "hp"):
                 at = cols(0 if name == "in" else 1 + n)
                 quant(ih_codes[:, g, at], ih_scales[:, g, at], grouped[key][:], E4M3X4)
@@ -282,10 +284,11 @@ def tile_grucell_v_kernel(
             for unit, operand in zip(units, quant_turned("darq", 4, dar_t[units])):
                 dar_q[unit] = operand
 
-        def pe_out0(i, banks=(6, 7), only=None):
+        def pe_out0(i, banks=(6, 7), only=None, passes=range(2 * KP)):
             for n in range(2) if only is None else (only - 1,):
-                o_ps[i, n] = bank(banks[n])
-                for k in range(2 * KP):
+                if passes[0] == 0:
+                    o_ps[i, n] = bank(banks[n])
+                for k in passes:
                     kp = k % KP
                     codes, scales = daz_q[i][kp] if k < KP else dar_q[i, kp]
                     gate = "z" if k < KP else "r"
@@ -461,7 +464,7 @@ def tile_grucell_v_kernel(
             if k >= 4:
                 take_words(S, ("g", k))
             s_negate_h(k + 1)
-            share = G_SHARE if k >= 4 else G_EARLY
+            share = H if k == CATCH else G_SHARE if k >= 4 else G_EARLY
             less_g(G, k, slice(0, share))
             if k == CATCH:
                 v_out0(k - 4)
@@ -478,7 +481,8 @@ def tile_grucell_v_kernel(
             pe_d(both(b + 1))
             pe_e(k)
             take_words(S, ("d", both(b)))
-            less_g(V, k, slice(share, H))
+            if share < H:
+                less_g(V, k, slice(share, H))
             if k + 3 < TILES:
                 load_g(k + 3)
             v_mr(b + 1)
@@ -554,41 +558,47 @@ def tile_grucell_v_kernel(
         v_mr(6, 2, cols(1))
         q_dar(first)
         v_hm(6, 2, cols(1))
+        out1(S, 4)
+        pe_out0(6, (1, 6), 1, range(3))
         v_dr(first[:1])
         v_dar(second, 4)
-        for b in range(4, 7):
+        for b in range(5, 8):
             out1(S, b)
+            if b == 6:
+                pe_out0(6, (1, 6), 2, range(3))
         take_words(S, ("d", second))
-        out1(S, 7)
+        il(S, ("in", 1, 0), hi=S_INPUTS)
+        ring = (2, 4, 7, 5)
+        il(V, ("dar", 1, 1), hi=NB // 2)
         qe(("dar", 0, 1))
-        il(V, ("dar", 1, 1))
-        q_dar(second)
-        pe_out0(6, (4, 5), 1)
-        qe(("dar", 1, 1))
-        v_dr(second[:1])
-        add_dr(G, 6)
-        for b in range(8, 12):
+        qe(("dar", 1, 1), hi=NB // 2)
+        for b in range(8, 11):
             pe_out1(b, ring[b % 4])
-        pe_out0(6, (4, 5), 2)
-        il(S, ("in", 0, 0))
-        il(S, ("in", 1, 0))
-        for b in range(8, 12):
-            out1(V, b)
-            pe_out1(b + 4, ring[b % 4])
-        v_out0(6)
+        il(V, ("dar", 1, 1), lo=NB // 2)
+        v_dr(second[:1])
+        pe_out1(11, ring[3])
+        qe(("dar", 1, 1), lo=NB // 2)
+        il(V, ("in", 0, 0))
+        il(V, ("in", 1, 0), lo=S_INPUTS)
         qe(("in", 0, 0))
         qe(("in", 1, 0))
-        less_g(V, 7, slice(G_SHARE, H))
-        q_pair(8, slice(1, 2))
-        for b in range(12, 16):
+        q_dar(second)
+        add_dr(G, 6)
+        for b in range(8, 16):
             out1(S, b)
             pe_out1(b + 4, ring[b % 4])
+            if b == 13:
+                pe_out0(6, passes=range(3, 4))
         v_dr(both(7))
-        add_dr(G, 7)
         for b in range(16, 20):
-            out1(V if b == 19 else S, b)
+            out1(V if b == 18 else S, b)
             pe_out1(b + 4, ring[b % 4])
+        less_g(V, 7, slice(G_SHARE, H))
+        q_pair(8, slice(1, 2))
+        add_dr(G, 7)
         pe_out0(7, (3, 0))
-        for b in range(20, 24):
-            out1(V if b % 2 else S, b)
+        out1(S, 20)
+        v_out0(6)
+        for b in range(21, 24):
+            out1(V if b == 23 else S, b)
         v_out0(7)

from contextlib import ExitStack
import math

import concourse.mybir as mybir
from concourse.masks import make_identity

F32 = mybir.dt.float32
BF16 = mybir.dt.bfloat16
U32 = mybir.dt.uint32
U8 = mybir.dt.uint8
E4M3X4 = mybir.dt.float8_e4m3fn_x4
E5M2X4 = mybir.dt.float8_e5m2_x4
ACT = mybir.ActivationFunctionType
ALU = mybir.AluOpType

B, I, H = 1024, 512, 1024
C = I + H
FLOPS = 2 * B * H * H + 2 * B * 2 * H * H + 2 * H * B * C
BYTES = 2 * (B * I + B * H + 3 * H * H + B * H) + 4 * 3 * B * H + 4 * (B * H + H * C)

P = 128
PACK = 4
NB = 512
KP = 2
TILES = 8
G_SHARE = 896
G_EARLY = 640
G_FIRST = 384
V_LAST = 256
S_INPUTS = 192
CATCH = 6

SIXTH = 1.0 / 6.0
EDGE = 1.0 + 2.0 ** -8
ROOT_1 = math.sqrt(EDGE) * (1.0 + 2.0 ** -22)
ROOT_3 = ROOT_1 / 3.0


def tile_grucell_v_kernel(
    tc, inputs, h_prev, W_z, b_z, W_r, b_r, W_h, b_h, a_z, a_r, a_h, grad_out, out_0, out_1
):
    nc = tc.nc
    V, S, G, PE, Q = nc.vector, nc.scalar, nc.gpsimd, nc.tensor, nc.sync

    def tokens(x):
        return x.rearrange("(g p j) w -> p g j w", g=KP, j=PACK)

    az_h, ar_h, ah_h = tokens(a_z), tokens(a_r), tokens(a_h)
    g_h, h_h, in_h, o0_h = tokens(grad_out), tokens(h_prev), tokens(inputs), tokens(out_0)
    w_h = {n: w[:, I:].rearrange("(k p j) c -> p k j c", k=KP, j=PACK) for n, w in (("h", W_h), ("z", W_z), ("r", W_r))}

    with ExitStack() as ctx:
        pool = ctx.enter_context(tc.tile_pool(name="sb", bufs=1))
        psum = ctx.enter_context(tc.psum_pool(name="ps", bufs=1))
        ctx.enter_context(tc.manual_schedule())

        def sb(shape, dt, tag, bufs=1):
            return pool.tile(shape, dt, name=tag, tag=tag, bufs=bufs, align_bytes=64)

        def bank(n):
            return psum.tile([P, NB], F32, name="bank%d" % n, tag="bank%d" % n, bufs=1)

        def cols(n, width=NB):
            return slice(n * width, (n + 1) * width)

        seed, half = sb([P, 1], F32, "seed"), sb([P, 1], F32, "half")
        ident = sb([P, P], F32, "ident")

        w_scales = {n: sb([P, KP, H], U8, "ws" + n) for n in "hzr"}
        w_codes = {n: sb([P, KP, H], U32, "wc" + n) for n in "hzr"}
        ih_codes, ih_scales = sb([P, KP, C], U32, "ihc"), sb([P, KP, C], U8, "ihs")
        tok_codes, tok_scales = sb([P, KP, H], U32, "tokc"), sb([P, KP, H], U8, "toks")

        az, ah, gg, raw, h_nat, terms, grouped = {}, {}, {}, {}, {}, {}, {}

        pair = {}
        qh, qz, clip, neg_h, e_ps, dz2_t, gm_t, daz_t, words_ps = {}, {}, {}, {}, {}, {}, {}, {}, {}
        ar, dar, d_ps, dar_t, o_ps, dz2_q, daz_q, dar_q = {}, {}, {}, {}, {}, {}, {}, {}

        def load_az(i, at=slice(0, H)):
            if at.start == 0:
                az[i] = sb([P, H], F32, "az", 2)
            Q.dma_start(out=az[i][:, at], in_=az_h[:, i // 4, i % 4, at])

        def load_ah(i):
            ah[i] = sb([P, H], F32, "ah", 2)
            Q.dma_start(out=ah[i][:], in_=ah_h[:, i // 4, i % 4, :])

        def load_g(i):
            gg[i] = sb([P, H], BF16, "gg", 3)
            Q.dma_start(out=gg[i][:], in_=g_h[:, i // 4, i % 4, :])

        def load_h(g, t0, t1):
            if t0 == 0:
                h_nat[g] = sb([P, PACK, H], BF16, "hnat", 2)
            Q.dma_start(out=h_nat[g][:, t0:t1, :], in_=h_h[:, g, t0:t1, :])

        def load_w(n, kp, at=slice(0, H)):
            if at.start == 0:
                raw[n, kp] = sb([P, PACK, H], BF16, "raw", 2)
            Q.dma_start(out=raw[n, kp][:, :, at], in_=w_h[n][:, kp, :, at])

        def load_inputs():
            raw["in"] = sb([P, KP, PACK, I], BF16, "raw", 2)
            Q.dma_start(out=raw["in"][:], in_=in_h)

        def load_ar(i):
            ar[i] = sb([P, H], F32, "ar", 3)
            Q.dma_start(out=ar[i][:], in_=ar_h[:, i // 4, i % 4, :])

        def quant(codes, scales, src, fmt):
            V.quantize_mx(out=codes.bitcast(fmt), scales=scales, in_=src)

        def interleave(eng, dst, src):
            dst = dst.rearrange("p (c i t) -> p c t i", i=4, t=PACK)
            src = src.rearrange("p t (c i) -> p c t i", i=4)
            if eng is S:
                S.copy(out=dst, in_=src)
            else:
                V.tensor_copy(out=dst, in_=src)

        def il(eng, key, tag=("grouped", 3), lo=0, hi=NB):
            name, g, n = key
            if lo == 0:
                grouped[key] = sb([P, NB * PACK], BF16, *tag)
            if name == "in":
                src = raw["in"][:, g]
            else:
                src = {"hp": h_nat, "dar": dar}[name][g] if name in ("hp", "dar") else raw[name, g]
                src = src[:, :, cols(n)]
            interleave(eng, grouped[key][:, lo * PACK:hi * PACK], src[:, :, lo:hi])

        def qe(key, lo=0, hi=NB):
            name, g, n = key
            if name == "dar":
                at = slice(n * NB + lo, n * NB + hi)
                quant(tok_codes[:, g, at], tok_scales[:, g, at], grouped[key][:, lo * PACK:hi * PACK], E5M2X4)
            elif name in ("in", "hp"):
                at = cols(0 if name == "in" else 1 + n)
                quant(ih_codes[:, g, at], ih_scales[:, g, at], grouped[key][:], E4M3X4)
            else:
                quant(w_codes[name][:, g, cols(n)], w_scales[name][:, g, cols(n)], grouped[key][:], E4M3X4)

        def pair_half(j, which):
            if j not in pair:
                pair[j] = sb([P, 2, KP, P, PACK], BF16, "pair", 2)
            return pair[j][:, which]

        def q_pair(j, which=slice(0, 2)):
            codes, scales = sb([P, 2, KP, P], U32, "pairc", 5), sb([P, 2, KP, P], U8, "pairs", 5)
            quant(codes[:, which].rearrange("p w k r -> p (w k r)"), scales[:, which].rearrange("p w k r -> p (w k r)"),
                  pair[j][:, which].rearrange("p w k r s -> p (w k r s)"), E5M2X4)
            for w in range(which.start, which.stop):
                (dz2_q, daz_q)[w][j - w] = [(codes[:, w, k], scales[:, w, k]) for k in range(KP)]

        def quant_turned(tag, bufs, src):
            codes, scales = sb([P, 2, P], U32, tag + "c", bufs), sb([P, 2, P], U8, tag + "s", bufs)
            quant(codes[:].rearrange("p k r -> p (k r)"), scales[:].rearrange("p k r -> p (k r)"),
                  src[:].rearrange("p k r s -> p (k r s)"), E5M2X4)
            return [(codes[:, k], scales[:, k]) for k in range(2)]

        def term(i):
            return terms[i][:]

        def s_p(i, at=slice(0, H)):
            if at.start == 0:
                terms[i] = sb([P, H], F32, "terms", 7)
            S.activation(out=term(i)[:, at], in_=az[i][:, at], func=ACT.Relu, bias=half[:], scale=-SIXTH)

        def s_qh(i):
            qh[i] = sb([P, H], BF16, "qh", 2)
            S.activation(out=qh[i][:], in_=ah[i][:], func=ACT.Square, scale=ROOT_1)

        def s_qz(i, at=slice(0, H)):
            if at.start == 0:
                qz[i] = sb([P, H], BF16, "qz", 2)
            S.activation(out=qz[i][:, at], in_=az[i][:, at], func=ACT.Square, scale=ROOT_3)

        def s_negate_h(i):
            neg_h[i] = sb([P, PACK, KP * P], F32, "negh", 2)
            S.activation(out=neg_h[i][:].rearrange("p s (b e) -> p b s e", e=4),
                         in_=h_nat[i // 4][:, i % 4, :].rearrange("p (b e s) -> p b s e", e=4, s=PACK), func=ACT.Copy, scale=-1.0)

        def v_clip(i):
            clip[i] = sb([P, PACK, KP * P], F32, "clip", 2)
            V.tensor_scalar(out=clip[i][:].rearrange("p s n -> p n s"), in0=ah[i][:].rearrange("p (n s) -> p n s", s=PACK),
                            scalar1=-1.0, scalar2=1.0, op0=ALU.max, op1=ALU.min)

        def pe_e(i, first_bank=0):
            for kp in range(KP):
                e_ps[i, kp] = bank(first_bank + kp)
                for s in range(PACK):
                    for src, first in ((clip, True), (neg_h, False)):
                        PE.matmul(out=e_ps[i, kp][:, cols(s, P)], lhsT=src[i][:, s, cols(kp, P)], rhs=ident[:],
                                  start=first, stop=not first, is_transpose=True)

        def turn_words(key, halves, n):
            words_ps[key] = bank(n)
            for k, src in enumerate(halves):
                w = src.bitcast(F32)
                for u in range(2):
                    PE.transpose(words_ps[key][:, cols(2 * k + u, P)], w[:, u::2], ident[:])

        def copy(eng, dst, src):
            if eng is S:
                S.copy(out=dst, in_=src)
            else:
                V.tensor_copy(out=dst, in_=src)

        def take_words(eng, key):
            if key[0] == "a":
                out = pair_half(key[1], 0)
            else:
                out = sb([P, KP, P, PACK], BF16, "turned" + key[0], 2)[:]
                {"g": gm_t, "d": dar_t}[key[0]][key[1]] = out
            copy(eng, out.bitcast(F32), words_ps[key][:].rearrange("p (k u r) -> p k r u", k=KP, u=2))

        def v_u(i, at=slice(0, H)):
            y = term(i)[:, at]
            V.scalar_tensor_tensor(out=y, in0=y, scalar=1.0, in1=gg[i][:, at], op0=ALU.min, op1=ALU.mult)

        def v_dz2(i):
            V.scalar_tensor_tensor(out=qh[i][:], in0=qh[i][:], scalar=EDGE, in1=term(i), op0=ALU.is_lt, op1=ALU.mult)
            turn_words(("a", i), [qh[i][:, cols(n)] for n in range(2)], 2)

        def v_mz(i, at=slice(0, H)):
            V.tensor_scalar(out=qz[i][:, at], in0=qz[i][:, at], scalar1=EDGE, scalar2=None, op0=ALU.is_lt)

        def v_gm(i, at_bank=3):
            V.tensor_tensor(out=qz[i][:], in0=qz[i][:], in1=gg[i][:], op=ALU.mult)
            turn_words(("g", i), [qz[i][:, cols(n)] for n in range(2)], at_bank)

        def less_g(eng, i, at=slice(0, H)):
            y = term(i)[:, at]
            eng.tensor_tensor(out=y, in0=y, in1=gg[i][:, at], op=ALU.subtract)

        def v_daz(i, kp):
            V.scalar_tensor_tensor(out=pair_half(i + 1, 1)[:, kp], in0=e_ps[i, kp][:].rearrange("p (s r) -> p r s", s=PACK),
                                   scalar=-SIXTH, in1=gm_t[i][:, kp], op0=ALU.mult, op1=ALU.mult)

        def s_qr(i, at=slice(0, H)):
            if i % 4 == 0:
                dar[i // 4] = sb([P, PACK, H], BF16, "dar", 2)
            S.activation(out=dar[i // 4][:, i % 4, at], in_=ar[i][:, at], func=ACT.Square, scale=ROOT_3)

        def s_r(i, at=slice(0, H)):
            S.activation(out=ar[i][:, at], in_=ar[i][:, at], func=ACT.Relu, bias=half[:], scale=SIXTH)

        def v_mr(i, tiles=1, at=slice(0, H)):
            y = dar[i // 4][:, i % 4:i % 4 + tiles, at]
            V.tensor_scalar(out=y, in0=y, scalar1=EDGE, scalar2=None, op0=ALU.is_lt)

        def v_hm(i, tiles=1, at=slice(0, H)):
            y = dar[i // 4][:, i % 4:i % 4 + tiles, at]
            V.tensor_tensor(out=y, in0=y, in1=h_nat[i // 4][:, i % 4:i % 4 + tiles, at], op=ALU.mult)

        def pe_d(units, banks=(4, 5)):
            for (i, n), at_bank in zip(units, banks):
                d_ps[i, n] = bank(at_bank)
                for kp in range(KP):
                    codes, scales = dz2_q[i][kp]
                    PE.matmul_mx(
                        out=d_ps[i, n][:], lhsT=codes.bitcast(E5M2X4), lhsT_scale=scales,
                        rhs=w_codes["h"][:, kp, cols(n)].bitcast(E4M3X4), rhs_scale=w_scales["h"][:, kp, cols(n)],
                        start=kp == 0, stop=kp == KP - 1,
                    )

        def v_dr(units):
            for i, n in units:
                r = ar[i][:, cols(n)]
                V.scalar_tensor_tensor(out=r, in0=r, scalar=1.0, in1=d_ps[i, n][:], op0=ALU.min, op1=ALU.mult)

        def add_dr(eng, i, at=slice(0, H)):
            y = terms[i][:, at]
            eng.tensor_tensor(out=y, in0=ar[i][:, at], in1=y, op=ALU.subtract)

        def v_dar(units, at_bank=2):
            for i, n in units:
                y = dar[i // 4][:, i % 4, cols(n)]
                V.scalar_tensor_tensor(out=y, in0=d_ps[i, n][:], scalar=SIXTH, in1=y, op0=ALU.mult, op1=ALU.mult)
            turn_words(("d", units), [dar[i // 4][:, i % 4, cols(n)] for i, n in units], at_bank)

        def q_dar(units):
            for unit, operand in zip(units, quant_turned("darq", 4, dar_t[units])):
                dar_q[unit] = operand

        def pe_out0(i, banks=(6, 7), only=None, passes=range(2 * KP)):
            for n in range(2) if only is None else (only - 1,):
                if passes[0] == 0:
                    o_ps[i, n] = bank(banks[n])
                for k in passes:
                    kp = k % KP
                    codes, scales = daz_q[i][kp] if k < KP else dar_q[i, kp]
                    gate = "z" if k < KP else "r"
                    PE.matmul_mx(
                        out=o_ps[i, n][:], lhsT=codes.bitcast(E5M2X4), lhsT_scale=scales,
                        rhs=w_codes[gate][:, kp, cols(n)].bitcast(E4M3X4), rhs_scale=w_scales[gate][:, kp, cols(n)],
                        start=k == 0, stop=k == 2 * KP - 1,
                    )

        def v_out0(i):
            for n in range(2):
                y = terms[i][:, cols(n)]
                V.tensor_tensor(out=y, in0=o_ps[i, n][:], in1=y, op=ALU.add)
                if i == TILES - 1:
                    Q.dma_start(out=o0_h[:, i // 4, i % 4, cols(n)], in_=y)
            if i < TILES - 1:
                Q.dma_start(out=o0_h[:, i // 4, i % 4, :], in_=term(i))

        stage = {}

        blocks = ([(m, n) for n in (1, 2) for m in range(4)] + [(m, n) for m in range(4, 8) for n in (1, 2)]
                  + [(m, 0) for m in range(8)])

        def pe_out1(b, at_bank):
            m, n = blocks[b]
            o_ps[b] = bank(at_bank)
            for g in range(KP):
                PE.matmul_mx(
                    out=o_ps[b][:],
                    lhsT=tok_codes[:, g, cols(m, P)].bitcast(E5M2X4), lhsT_scale=tok_scales[:, g, cols(m, P)],
                    rhs=ih_codes[:, g, cols(n)].bitcast(E4M3X4), rhs_scale=ih_scales[:, g, cols(n)],
                    start=g == 0, stop=g == KP - 1,
                )

        def out1(eng, b):
            m, n = blocks[b]
            if m < 4 or n == 0:
                if b % 2 == 0:
                    stage[b // 2] = sb([P, 2, NB], F32, ("az", "ah", "clip", "negh")[b // 2 % 4], 2)
                dst = stage[b // 2][:, b % 2, :]
                copy(eng, dst, o_ps[b][:])
                Q.dma_start(out=out_1[cols(m, P), cols(n)], in_=dst)
            else:
                if n == 1:
                    stage["row", m] = sb([P, 2 * NB], F32, "terms", 7)
                copy(eng, stage["row", m][:, cols(n - 1)], o_ps[b][:])
                if n == 2:
                    Q.dma_start(out=out_1[cols(m, P), NB:], in_=stage["row", m][:])

        def both(i):
            return ((i, 0), (i, 1))

        def front(k, words=False, passes=False):
            v_clip(k)
            if words:
                q_dar(both(k - 3))
            if passes:
                pe_out0(k - 3, only=1)
            if k + 2 < TILES:
                load_ah(k + 2)
            v_u(k)
            v_mz(k)
            q_pair(k - 1, slice(0, 2 if k > 1 else 1))
            v_dz2(k)
            v_gm(k)

        def turned(k):
            take_words(S, ("a", k))
            take_words(S, ("g", k))

        def daz(k):
            v_daz(k, 0)
            v_daz(k, 1)

        load_az(0)
        load_ah(0)
        load_g(0)
        load_h(0, 0, 1)
        load_az(1)
        load_w("h", 0)
        load_ah(1)
        load_h(0, 1, 2)
        load_g(1)
        load_ar(0)
        load_w("h", 1)
        V.memset(seed[:], 0.5)
        S.activation(out=half[:], in_=seed[:], func=ACT.Relu)
        make_identity(nc, ident[:])
        s_p(0)
        s_qh(0)
        s_qz(0)
        load_az(2)
        v_clip(0)
        load_ah(2)
        v_u(0)
        v_dz2(0)
        v_mz(0)
        less_g(V, 0)
        v_gm(0)
        load_g(2)
        s_p(1)
        s_qz(1)
        s_negate_h(0)
        pe_e(0)
        turned(0)
        s_qh(1)
        s_negate_h(1)
        il(V, ("h", 0, 0))
        il(V, ("h", 0, 1))
        qe(("h", 0, 0))
        qe(("h", 0, 1))
        load_w("z", 0)
        load_h(0, 2, PACK)
        load_ar(1)
        load_az(3)
        s_qr(0)
        s_r(0)
        il(S, ("h", 1, 0))

        front(1)
        less_g(G, 1, slice(0, G_FIRST))
        daz(0)
        il(V, ("h", 1, 1))
        load_w("z", 1)
        load_g(3)
        s_p(2)
        s_qh(2)
        s_qz(2)
        load_az(4)
        turned(1)
        il(S, ("z", 0, 0))
        s_negate_h(2)
        pe_e(1)
        qe(("h", 1, 0))
        less_g(V, 1, slice(G_FIRST, H))
        load_g(4)
        v_mr(0)
        qe(("h", 1, 1))
        pe_d(both(0))
        v_hm(0)
        load_ar(2)
        load_h(1, 0, PACK)

        extra = {
            2: ((S, ("z", 0, 1)), (V, ("z", 1, 0)), (S, ("z", 1, 1))),
            3: ((V, ("r", 0, 0)), (S, ("r", 0, 1)), (S, ("r", 1, 0))),
            4: (),
            5: ((S, ("hp", 0, 0)),),
            6: ((S, ("hp", 1, 0)),),
        }
        first, second = ((6, 0), (7, 0)), ((6, 1), (7, 1))
        waiting = [("z", 0, 0)]
        for k in range(2, TILES - 1):
            b = k - 2
            if k == 4:
                qe(waiting.pop(0))
                il(S, ("r", 1, 1), hi=NB - V_LAST)
            s_qr(b + 1)
            s_p(k + 1)
            s_qh(k + 1)
            s_qz(k + 1)
            if k + 3 < TILES:
                load_az(k + 3)
            front(k, k >= CATCH, k > CATCH)
            if k == 4:
                il(V, ("r", 1, 1), lo=NB - V_LAST)
                qe(waiting.pop(0))
                qe(("r", 1, 0))
                qe(("r", 1, 1))
                pe_out0(0)
            take_words(S, ("a", k))
            s_r(b + 1)
            if k >= 4:
                take_words(S, ("g", k))
            s_negate_h(k + 1)
            share = H if k == CATCH else G_SHARE if k >= 4 else G_EARLY
            less_g(G, k, slice(0, share))
            if k == CATCH:
                v_out0(k - 4)
                pe_out0(k - 3)
            v_dr(both(b))
            add_dr(G, b)
            v_dar(both(b))
            load_ar(b + 3)
            daz(k - 1)
            if k >= 4:
                v_out0(k - 4 if k < CATCH else k - 3)
            else:
                take_words(V, ("g", k))
            pe_d(both(b + 1))
            pe_e(k)
            take_words(S, ("d", both(b)))
            if share < H:
                less_g(V, k, slice(share, H))
            if k + 3 < TILES:
                load_g(k + 3)
            v_mr(b + 1)
            for key in waiting:
                qe(key)
            waiting = []
            if 0 < b < CATCH - 2:
                q_dar(both(b - 1))
            if k == 3:
                il(V, ("r", 0, 0))
            v_hm(b + 1)
            for eng, key in extra[k]:
                if key != ("r", 0, 0):
                    il(eng, key)
                if key != ("r", 1, 0):
                    waiting.append(key)
                if key[2] == 1 and key[0] == "z":
                    load_w("r", key[1])
                if key == ("r", 0, 1):
                    load_inputs()
            if 4 <= k < CATCH:
                pe_out0(k - 3)

        s_qr(6)
        il(S, ("dar", 0, 0))
        il(S, ("hp", 0, 1), ("raw", 2))
        front(7, True, True)
        pe_out0(4, only=2)
        take_words(S, ("a", 7))
        s_qr(7)
        take_words(S, ("g", 7))
        less_g(G, 7, slice(0, G_SHARE))
        v_dr(both(5))
        add_dr(G, 5)
        v_dar(both(5))
        pe_d(both(6))
        daz(6)
        pe_e(7)
        v_out0(4)
        q_pair(7, slice(0, 1))
        pe_d(first[1:], (3,))
        take_words(S, ("d", both(5)))
        qe(("hp", 1, 0))
        il(S, ("hp", 1, 1))
        v_mr(6, 2, cols(0))
        qe(("dar", 0, 0))
        il(S, ("dar", 0, 1))
        q_dar(both(5))
        v_hm(6, 2, cols(0))
        pe_out0(5)
        q_pair(7, slice(1, 2))

        s_r(6)
        v_dar(first)
        v_daz(7, 0)
        il(V, ("dar", 1, 0))
        take_words(S, ("d", first))
        v_daz(7, 1)
        pe_d(second[1:], (0,))
        qe(("dar", 1, 0))
        s_r(7)
        ring = (1, 2, 6, 7)
        pe_out1(0, ring[0])
        pe_out1(1, ring[1])
        v_out0(5)
        pe_out1(2, ring[2])
        pe_out1(3, ring[3])
        qe(("hp", 0, 1))
        qe(("hp", 1, 1))
        for b in range(4):
            out1(S, b)
            pe_out1(b + 4, ring[b])
        v_mr(6, 2, cols(1))
        q_dar(first)
        v_hm(6, 2, cols(1))
        out1(S, 4)
        pe_out0(6, (1, 6), 1, range(3))
        v_dr(first[:1])
        v_dar(second, 4)
        for b in range(5, 8):
            out1(S, b)
            if b == 6:
                pe_out0(6, (1, 6), 2, range(3))
        take_words(S, ("d", second))
        il(S, ("in", 1, 0), hi=S_INPUTS)
        ring = (2, 4, 7, 5)
        il(V, ("dar", 1, 1), hi=NB // 2)
        qe(("dar", 0, 1))
        qe(("dar", 1, 1), hi=NB // 2)
        for b in range(8, 11):
            pe_out1(b, ring[b % 4])
        il(V, ("dar", 1, 1), lo=NB // 2)
        v_dr(second[:1])
        pe_out1(11, ring[3])
        qe(("dar", 1, 1), lo=NB // 2)
        il(V, ("in", 0, 0))
        il(V, ("in", 1, 0), lo=S_INPUTS)
        qe(("in", 0, 0))
        qe(("in", 1, 0))
        q_dar(second)
        add_dr(G, 6)
        for b in range(8, 16):
            out1(S, b)
            pe_out1(b + 4, ring[b % 4])
            if b == 13:
                pe_out0(6, passes=range(3, 4))
        v_dr(both(7))
        for b in range(16, 20):
            out1(V if b == 18 else S, b)
            pe_out1(b + 4, ring[b % 4])
        less_g(V, 7, slice(G_SHARE, H))
        q_pair(8, slice(1, 2))
        add_dr(G, 7)
        pe_out0(7, (3, 0))
        out1(S, 20)
        v_out0(6)
        for b in range(21, 24):
            out1(V if b == 23 else S, b)
        v_out0(7)
